import numpy as np
import ml_dtypes


def mxq(x, axis, fmt="e4m3"):
    dtype, down = {"e4m3": (ml_dtypes.float8_e4m3fn, 7), "e5m2": (ml_dtypes.float8_e5m2, 14)}[fmt]
    v = np.moveaxis(np.asarray(x, np.float32).astype(ml_dtypes.bfloat16).astype(np.float64), axis, -1)
    blocks = v.reshape(v.shape[:-1] + (-1, 32))
    amax = np.abs(blocks).max(-1, keepdims=True)
    byte = np.maximum(np.where(amax > 0, np.frexp(amax)[1] - 1 + 127, 0) - down, 1)
    scale = np.exp2(byte - 127.0)
    codes = (blocks / scale).astype(np.float32).astype(dtype).astype(np.float64)
    return np.moveaxis((codes * scale).reshape(v.shape), -1, axis)


WIDE = False


def mx_kscale(k):
    if not WIDE:
        return np.ones(k)
    levels = np.array([10, -10, 5, -5, 0])
    if k % 512:
        return np.exp2(np.random.permutation(np.resize(levels, k // 32))).repeat(32)
    a = np.empty((k // 512, 16))
    for p in range(k // 512):
        a[p, :8] = np.random.permutation(np.resize(levels, 8))
        for g in range(8):
            far = levels[np.abs(levels - a[p, g]) >= 10]
            a[p, g + 8] = far[np.random.randint(len(far))]
    return np.exp2(a.ravel()).repeat(32)


BF16 = ml_dtypes.bfloat16


def bf(x):
    return np.asarray(x, np.float32).astype(BF16)


def f64(x):
    return np.asarray(x).astype(np.float64)


LQ, LK, D, H, DK, DV = 1024, 1024, 2048, 4, 128, 128
HV = H * DV
LN_EPS = 1e-5


def setup_inputs():
    s = mx_kscale(HV)
    return {"attn_out": bf(np.random.standard_normal((H, LQ, DV)) * 0.7 * s.reshape(H, DV)[:, None, :]),
            "residual": bf(np.random.standard_normal((LQ, D))),
            "proj_w": bf(np.random.standard_normal((HV, D)) / np.sqrt(HV) / s[:, None]),
            "proj_b": bf(np.random.standard_normal(D) * 0.3),
            "ln_g": bf(1.0 + 0.1 * np.random.standard_normal(D)),
            "ln_b": bf(0.1 * np.random.standard_normal(D))}


def reference(attn_out, residual, proj_w, proj_b, ln_g, ln_b):
    x = f64(attn_out).transpose(1, 0, 2).reshape(LQ, HV)
    y = (mxq(x, 1, "e4m3") @ mxq(f64(proj_w), 0, "e4m3")) + f64(proj_b) + f64(residual)
    mu = y.mean(-1, keepdims=True)
    var = ((y - mu) ** 2).mean(-1, keepdims=True)
    return (y - mu) / np.sqrt(var + LN_EPS) * f64(ln_g) + f64(ln_b)

@@ -1,0 +1,221 @@
+from contextlib import ExitStack
+
+import concourse.mybir as mybir
+from concourse.masks import make_identity
+
+F32 = mybir.dt.float32
+BF16 = mybir.dt.bfloat16
+U32 = mybir.dt.uint32
+U8 = mybir.dt.uint8
+FP8X4 = mybir.dt.float8_e4m3fn_x4
+ALU = mybir.AluOpType
+ACT = mybir.ActivationFunctionType
+AX = mybir.AxisListType
+
+P = 128
+H = 4
+DV = 128
+LQ = 1024
+D = 2048
+NT = LQ // P
+NF = D // P
+BANK = 512
+NC = D // BANK
+F_PER_CHUNK = BANK // P
+TG = BANK // P
+NG = NT // TG
+LN_EPS = 1e-5
+
+FLOPS = 2 * LQ * H * DV * D
+
+
+def tile_multiheadattention_pb_kernel(tc, attn_out, residual, proj_w, proj_b, ln_g, ln_b, out):
+    nc = tc.nc
+    with ExitStack() as ctx:
+        keep = ctx.enter_context(tc.tile_pool(name="keep", bufs=1))
+        rows = ctx.enter_context(tc.tile_pool(name="rows", bufs=NG))
+        work = ctx.enter_context(tc.tile_pool(name="work", bufs=3))
+        small = ctx.enter_context(tc.tile_pool(name="small", bufs=4))
+        psum_f = ctx.enter_context(tc.psum_pool(name="psum_f", bufs=4))
+        psum_t = ctx.enter_context(tc.psum_pool(name="psum_t", bufs=4))
+
+        bias_rows = keep.tile([P, P], BF16)
+        nc.vector.memset(bias_rows[:], 0.0)
+        nc.sync.dma_start(out=bias_rows[0:NF, :], in_=proj_b.rearrange("(j q) -> j q", q=P))
+        x_raw = keep.tile([P, H, NT, DV], BF16)
+        x_view = attn_out.rearrange("h (p t) j -> p h t j", t=NT)
+        w_raw = keep.tile([P, H, D], BF16)
+        w_view = proj_w.rearrange("(q i) n -> q i n", i=H)
+        r_sb = keep.tile([P, NT, D], BF16)
+        r_view = residual.rearrange("(p t) n -> p t n", t=NT)
+        gain_bc = keep.tile([P, D], BF16)
+        shift_bc = keep.tile([P, D], BF16)
+
+        def load_x(g):
+            tiles = slice(g * TG, (g + 1) * TG)
+            nc.sync.dma_start(
+                out=x_raw[:, :, tiles, :].rearrange("p h t j -> p h (t j)"),
+                in_=x_view[:, :, tiles, :].rearrange("p h t j -> p h (t j)"),
+            )
+
+        def load_w(c):
+            cols = slice(c * BANK, (c + 1) * BANK)
+            nc.sync.dma_start(out=w_raw[:, :, cols], in_=w_view[:, :, cols])
+
+        def load_r(g, c):
+            tiles = slice(g * TG, (g + 1) * TG)
+            cols = slice(c * BANK, (c + 1) * BANK)
+            nc.sync.dma_start(out=r_sb[:, tiles, cols], in_=r_view[:, tiles, cols])
+
+        load_x(0)
+        for c in range(NC):
+            load_w(c)
+            load_r(0, c)
+        load_x(1)
+        nc.sync.dma_start(out=gain_bc[:], in_=ln_g.partition_broadcast(P))
+        load_r(1, 0)
+        nc.sync.dma_start(out=shift_bc[:], in_=ln_b.partition_broadcast(P))
+        for c in range(1, NC):
+            load_r(1, c)
+
+        eps = keep.tile([P, 1], F32)
+        nc.vector.memset(eps[:], LN_EPS)
+        warm = keep.tile([P, 1], F32)
+        nc.scalar.activation(out=warm[:], in_=eps[:], func=ACT.Sqrt)
+        ident_b = keep.tile([P, P], BF16)
+        make_identity(nc, ident_b[:])
+        ident_f = keep.tile([P, P], F32)
+        make_identity(nc, ident_f[:])
+
+        x_words = keep.tile([P, NT, 2, P], F32)
+        x_grouped = keep.tile([P, NT, P, H], BF16, align_bytes=64)
+        x_codes = keep.tile([P, NT * P], U32, align_bytes=64)
+        x_scales = keep.tile([P, NT * P], U8, align_bytes=64)
+        w_grouped = keep.tile([P, D, H], BF16, align_bytes=64)
+        w_codes = keep.tile([P, D], U32, align_bytes=64)
+        w_scales = keep.tile([P, D], U8, align_bytes=64)
+        bias_col = keep.tile([P, NF], F32)
+        out_view = out.rearrange("(p t) n -> p t n", t=NT)
+
+        def quantise_x(g):
+            for t in range(g * TG, (g + 1) * TG):
+                nc.vector.tensor_copy(
+                    out=x_words[:, t, :, :].rearrange("p u (h a) -> p u h a", h=H),
+                    in_=x_raw[:, :, t, :].bitcast(F32).rearrange("p h (a u) -> p u h a", u=2),
+                )
+                xt = psum_t.tile([P, 2, P], F32, name="xt", tag="tok")
+                for u in range(2):
+                    nc.tensor.transpose(xt[:, u, :], x_words[:, t, u, :], ident_f[:])
+                nc.scalar.copy(
+                    out=x_grouped[:, t, :, :].rearrange("q p h -> q (p h)").bitcast(F32).rearrange("q (p u) -> q p u", u=2),
+                    in_=xt[:].rearrange("q u p -> q p u"),
+                )
+            toks = slice(g * BANK, (g + 1) * BANK)
+            nc.vector.quantize_mx(
+                out=x_codes[:, toks].bitcast(FP8X4),
+                scales=x_scales[:, toks],
+                in_=x_grouped[:, g * TG : (g + 1) * TG, :, :].rearrange("q t p h -> q (t p h)"),
+            )
+
+        def quantise_w(c):
+            cols = slice(c * BANK, (c + 1) * BANK)
+            w_rows = w_raw[:, :, cols].rearrange("q h n -> q n h")
+            if c % 2 == 0:
+                nc.vector.tensor_copy(out=w_grouped[:, cols, :], in_=w_rows)
+            else:
+                nc.scalar.copy(out=w_grouped[:, cols, :], in_=w_rows)
+            nc.vector.quantize_mx(
+                out=w_codes[:, cols].bitcast(FP8X4),
+                scales=w_scales[:, cols],
+                in_=w_grouped[:, cols, :].rearrange("q n h -> q (n h)"),
+            )
+
+        y_of = {}
+        sums_of = {}
+        zb_of = {}
+        neg_mean_of = {}
+
+        def multiply(g, c):
+            toks = slice(g * BANK, (g + 1) * BANK)
+            zb_of[g, c] = work.tile([P, F_PER_CHUNK, BANK], F32, name="zb")
+            for jj in range(F_PER_CHUNK):
+                j = c * F_PER_CHUNK + jj
+                feats = slice(j * P, (j + 1) * P)
+                z = psum_f.tile([P, BANK], F32, name="z")
+                nc.tensor.matmul_mx(
+                    out=z[:],
+                    lhsT=w_codes[:, feats].bitcast(FP8X4),
+                    lhsT_scale=w_scales[:, feats],
+                    rhs=x_codes[:, toks].bitcast(FP8X4),
+                    rhs_scale=x_scales[:, toks],
+                    start=True,
+                    stop=True,
+                )
+                nc.scalar.activation(
+                    out=zb_of[g, c][:, jj, :], in_=z[:], func=ACT.Identity, bias=bias_col[:, j : j + 1], scale=1.0
+                )
+
+        def add_residual(g, c):
+            if c == 0:
+                y_of[g] = rows.tile([P, TG, D], F32, name="y")
+                sums_of[g] = small.tile([P, TG, NC], F32, name="chunk_sums")
+            cols = slice(c * BANK, (c + 1) * BANK)
+            for i in range(TG):
+                zbt = psum_t.tile([P, BANK], F32, name="zbt", tag="tok")
+                for jj in range(F_PER_CHUNK):
+                    nc.tensor.transpose(zbt[:, jj * P : (jj + 1) * P], zb_of[g, c][:, jj, i * P : (i + 1) * P], ident_f[:])
+                nc.vector.scalar_tensor_tensor(
+                    out=y_of[g][:, i, cols],
+                    in0=zbt[:],
+                    scalar=0.0,
+                    in1=r_sb[:, g * TG + i, cols],
+                    op0=ALU.add,
+                    op1=ALU.add,
+                    accum_out=sums_of[g][:, i, c : c + 1],
+                )
+            if c == NC - 1:
+                row_sum = small.tile([P, TG], F32, name="row_sum")
+                nc.vector.tensor_reduce(out=row_sum[:], in_=sums_of[g][:], axis=AX.X, op=ALU.add)
+                neg_mean_of[g] = small.tile([P, TG], F32, name="neg_mean")
+                nc.vector.tensor_scalar_mul(out=neg_mean_of[g][:], in0=row_sum[:], scalar1=-1.0 / D)
+
+        def normalise(g, i):
+            neg_mean = neg_mean_of[g][:, i : i + 1]
+            squares = work.tile([P, D], BF16, name="squares")
+            sq_sum = small.tile([P, 1], F32, name="sq_sum")
+            nc.scalar.activation(
+                out=squares[:], in_=y_of[g][:, i, :], func=ACT.Square, bias=neg_mean, scale=1.0, accum_out=sq_sum[:]
+            )
+            std = small.tile([P, 1], F32, name="std")
+            nc.scalar.activation(out=std[:], in_=sq_sum[:], func=ACT.Sqrt, bias=eps[:], scale=1.0 / D)
+            o = work.tile([P, D], F32, name="o")
+            nc.vector.scalar_tensor_tensor(
+                out=o[:], in0=y_of[g][:, i, :], scalar=neg_mean, in1=gain_bc[:], op0=ALU.add, op1=ALU.mult
+            )
+            rstd = small.tile([P, 1], F32, name="rstd")
+            nc.vector.reciprocal(out=rstd[:], in_=std[:])
+            nc.vector.scalar_tensor_tensor(
+                out=o[:], in0=o[:], scalar=rstd[:], in1=shift_bc[:], op0=ALU.mult, op1=ALU.add
+            )
+            nc.sync.dma_start(out=out_view[:, g * TG + i, :], in_=o[:])
+
+        quantise_x(0)
+        bias_ps = psum_t.tile([P, P], BF16, tag="tok")
+        nc.tensor.transpose(bias_ps[:], bias_rows[:], ident_b[:])
+        nc.vector.tensor_copy(out=bias_col[:], in_=bias_ps[:, 0:NF])
+        quantise_w(0)
+        multiply(0, 0)
+        for g in range(NG + 1):
+            for c in range(NC):
+                if g == 0 and c + 1 < NC:
+                    quantise_w(c + 1)
+                if g + 1 < NG and c == 0:
+                    quantise_x(g + 1)
+                if c + 1 < NC and g < NG:
+                    multiply(g, c + 1)
+                if c + 1 == NC and g + 1 < NG:
+                    multiply(g + 1, 0)
+                if g < NG:
+                    add_residual(g, c)
+                if g >= 1:
+                    normalise(g - 1, c)

@@ -10,7 +10,6 @@ U8 = mybir.dt.uint8
 FP8X4 = mybir.dt.float8_e4m3fn_x4
 ALU = mybir.AluOpType
 ACT = mybir.ActivationFunctionType
-AX = mybir.AxisListType
 
 P = 128
 H = 4
@@ -22,8 +21,6 @@ NF = D // P
 BANK = 512
 NC = D // BANK
 F_PER_CHUNK = BANK // P
-TG = BANK // P
-NG = NT // TG
 LN_EPS = 1e-5
 
 FLOPS = 2 * LQ * H * DV * D
@@ -33,50 +30,54 @@ def tile_multiheadattention_pb_kernel(tc, attn_out, residual, proj_w, proj_b, ln
     nc = tc.nc
     with ExitStack() as ctx:
         keep = ctx.enter_context(tc.tile_pool(name="keep", bufs=1))
-        rows = ctx.enter_context(tc.tile_pool(name="rows", bufs=NG))
+        x_pool = ctx.enter_context(tc.tile_pool(name="x_pool", bufs=NT // 2))
         work = ctx.enter_context(tc.tile_pool(name="work", bufs=3))
+        cols_pool = ctx.enter_context(tc.tile_pool(name="cols_pool", bufs=8))
         small = ctx.enter_context(tc.tile_pool(name="small", bufs=4))
-        psum_f = ctx.enter_context(tc.psum_pool(name="psum_f", bufs=4))
-        psum_t = ctx.enter_context(tc.psum_pool(name="psum_t", bufs=4))
+        psum_z = ctx.enter_context(tc.psum_pool(name="psum_z", bufs=4))
+        psum_c = ctx.enter_context(tc.psum_pool(name="psum_c", bufs=2))
+        psum_o = ctx.enter_context(tc.psum_pool(name="psum_o", bufs=2))
 
-        bias_rows = keep.tile([P, P], BF16)
-        nc.vector.memset(bias_rows[:], 0.0)
-        nc.sync.dma_start(out=bias_rows[0:NF, :], in_=proj_b.rearrange("(j q) -> j q", q=P))
-        x_raw = keep.tile([P, H, NT, DV], BF16)
+        vec_rows = keep.tile([P, P], BF16)
+        nc.vector.memset(vec_rows[:], 0.0)
+        nc.sync.dma_start(out=vec_rows[0:NF, :], in_=proj_b.rearrange("(j q) -> j q", q=P))
+        nc.sync.dma_start(out=vec_rows[NF : 2 * NF, :], in_=ln_g.rearrange("(j q) -> j q", q=P))
+        x_raw = {}
         x_view = attn_out.rearrange("h (p t) j -> p h t j", t=NT)
         w_raw = keep.tile([P, H, D], BF16)
         w_view = proj_w.rearrange("(q i) n -> q i n", i=H)
         r_sb = keep.tile([P, NT, D], BF16)
         r_view = residual.rearrange("(p t) n -> p t n", t=NT)
-        gain_bc = keep.tile([P, D], BF16)
         shift_bc = keep.tile([P, D], BF16)
 
-        def load_x(g):
-            tiles = slice(g * TG, (g + 1) * TG)
+        def load_x(t0):
+            x_raw[t0] = x_pool.tile([P, H, 2, DV], BF16, name="x_pair")
             nc.sync.dma_start(
-                out=x_raw[:, :, tiles, :].rearrange("p h t j -> p h (t j)"),
-                in_=x_view[:, :, tiles, :].rearrange("p h t j -> p h (t j)"),
+                out=x_raw[t0][:].rearrange("p h t j -> p h (t j)"),
+                in_=x_view[:, :, t0 : t0 + 2, :].rearrange("p h t j -> p h (t j)"),
             )
 
         def load_w(c):
             cols = slice(c * BANK, (c + 1) * BANK)
             nc.sync.dma_start(out=w_raw[:, :, cols], in_=w_view[:, :, cols])
 
-        def load_r(g, c):
-            tiles = slice(g * TG, (g + 1) * TG)
-            cols = slice(c * BANK, (c + 1) * BANK)
-            nc.sync.dma_start(out=r_sb[:, tiles, cols], in_=r_view[:, tiles, cols])
+        def load_r(t):
+            nc.sync.dma_start(out=r_sb[:, t, :], in_=r_view[:, t, :])
 
+        load_w(0)
         load_x(0)
-        for c in range(NC):
-            load_w(c)
-            load_r(0, c)
-        load_x(1)
-        nc.sync.dma_start(out=gain_bc[:], in_=ln_g.partition_broadcast(P))
-        load_r(1, 0)
+        load_w(1)
+        load_w(2)
+        load_r(0)
+        load_w(3)
+        load_x(2)
+        load_r(1)
+        load_x(4)
+        load_r(2)
+        load_x(6)
         nc.sync.dma_start(out=shift_bc[:], in_=ln_b.partition_broadcast(P))
-        for c in range(1, NC):
-            load_r(1, c)
+        for t in range(3, NT):
+            load_r(t)
 
         eps = keep.tile([P, 1], F32)
         nc.vector.memset(eps[:], LN_EPS)
@@ -94,128 +95,245 @@ def tile_multiheadattention_pb_kernel(tc, attn_out, residual, proj_w, proj_b, ln
         w_grouped = keep.tile([P, D, H], BF16, align_bytes=64)
         w_codes = keep.tile([P, D], U32, align_bytes=64)
         w_scales = keep.tile([P, D], U8, align_bytes=64)
-        bias_col = keep.tile([P, NF], F32)
+        vec_col = keep.tile([P, 2 * NF], F32)
+        bias_bc = keep.tile([P, D], BF16)
         out_view = out.rearrange("(p t) n -> p t n", t=NT)
 
-        def quantise_x(g):
-            for t in range(g * TG, (g + 1) * TG):
-                nc.vector.tensor_copy(
-                    out=x_words[:, t, :, :].rearrange("p u (h a) -> p u h a", h=H),
-                    in_=x_raw[:, :, t, :].bitcast(F32).rearrange("p h (a u) -> p u h a", u=2),
-                )
-                xt = psum_t.tile([P, 2, P], F32, name="xt", tag="tok")
-                for u in range(2):
-                    nc.tensor.transpose(xt[:, u, :], x_words[:, t, u, :], ident_f[:])
-                nc.scalar.copy(
-                    out=x_grouped[:, t, :, :].rearrange("q p h -> q (p h)").bitcast(F32).rearrange("q (p u) -> q p u", u=2),
-                    in_=xt[:].rearrange("q u p -> q p u"),
-                )
-            toks = slice(g * BANK, (g + 1) * BANK)
-            nc.vector.quantize_mx(
-                out=x_codes[:, toks].bitcast(FP8X4),
-                scales=x_scales[:, toks],
-                in_=x_grouped[:, g * TG : (g + 1) * TG, :, :].rearrange("q t p h -> q (t p h)"),
+        def x_order(t):
+            nc.vector.tensor_copy(
+                out=x_words[:, t, :, :].rearrange("p u (h a) -> p u h a", h=H),
+                in_=x_raw[t - t % 2][:, :, t % 2, :].bitcast(F32).rearrange("p h (a u) -> p u h a", u=2),
             )
 
-        def quantise_w(c):
+        def x_grouped_pair(t0):
+            return x_grouped[:, t0 : t0 + 2, :, :].rearrange("q t p i -> q (t p i)")
+
+        def x_turn(t0):
+            xt = psum_c.tile([P, 2, 2, P], F32, name="xt", tag="c")
+            for t in range(2):
+                for u in range(2):
+                    nc.tensor.transpose(xt[:, t, u, :], x_words[:, t0 + t, u, :], ident_f[:])
+            nc.scalar.copy(
+                out=x_grouped_pair(t0).bitcast(F32).rearrange("q (t p u) -> q t p u", t=2, u=2),
+                in_=xt[:].rearrange("q t u p -> q t p u"),
+            )
+
+        def x_quantise(t0):
+            toks = slice(t0 * P, (t0 + 2) * P)
+            nc.vector.quantize_mx(out=x_codes[:, toks].bitcast(FP8X4), scales=x_scales[:, toks], in_=x_grouped_pair(t0))
+
+        def w_group(c, copy):
             cols = slice(c * BANK, (c + 1) * BANK)
-            w_rows = w_raw[:, :, cols].rearrange("q h n -> q n h")
-            if c % 2 == 0:
-                nc.vector.tensor_copy(out=w_grouped[:, cols, :], in_=w_rows)
-            else:
-                nc.scalar.copy(out=w_grouped[:, cols, :], in_=w_rows)
+            copy(out=w_grouped[:, cols, :], in_=w_raw[:, :, cols].rearrange("q i n -> q n i"))
+
+        def w_quantise(c):
+            cols = slice(c * BANK, (c + 1) * BANK)
             nc.vector.quantize_mx(
                 out=w_codes[:, cols].bitcast(FP8X4),
                 scales=w_scales[:, cols],
-                in_=w_grouped[:, cols, :].rearrange("q n h -> q (n h)"),
+                in_=w_grouped[:, cols, :].rearrange("q n i -> q (n i)"),
             )
 
-        y_of = {}
-        sums_of = {}
-        zb_of = {}
-        neg_mean_of = {}
+        def turn_vectors():
+            rows_ps = psum_o.tile([P, P], BF16, name="rows_ps", tag="o")
+            nc.tensor.transpose(rows_ps[:], vec_rows[:], ident_b[:])
+            nc.vector.tensor_copy(out=vec_col[:], in_=rows_ps[:, 0 : 2 * NF])
 
-        def multiply(g, c):
-            toks = slice(g * BANK, (g + 1) * BANK)
-            zb_of[g, c] = work.tile([P, F_PER_CHUNK, BANK], F32, name="zb")
+        def spread_bias(c):
+            spread = psum_z.tile([P, BANK], F32, name="spread", tag="z")
             for jj in range(F_PER_CHUNK):
                 j = c * F_PER_CHUNK + jj
-                feats = slice(j * P, (j + 1) * P)
-                z = psum_f.tile([P, BANK], F32, name="z")
-                nc.tensor.matmul_mx(
-                    out=z[:],
-                    lhsT=w_codes[:, feats].bitcast(FP8X4),
-                    lhsT_scale=w_scales[:, feats],
-                    rhs=x_codes[:, toks].bitcast(FP8X4),
-                    rhs_scale=x_scales[:, toks],
-                    start=True,
-                    stop=True,
+                nc.tensor.transpose(
+                    spread[:, jj * P : (jj + 1) * P], vec_col[:, j : j + 1].to_broadcast([P, P]), ident_f[:]
                 )
-                nc.scalar.activation(
-                    out=zb_of[g, c][:, jj, :], in_=z[:], func=ACT.Identity, bias=bias_col[:, j : j + 1], scale=1.0
+            nc.scalar.copy(out=bias_bc[:, c * BANK : (c + 1) * BANK], in_=spread[:])
+
+        rb_of = {}
+        y_of = {}
+        sums_of = {}
+        z_of = {}
+        neg_mean_of = {}
+        std_of = {}
+        centred_of = {}
+        scaled_of = {}
+        rstd_of = {}
+        back_of = {}
+        o_of = {}
+
+        def residual_and_bias(i):
+            rb_of[i] = work.tile([P, D], F32, name="rb")
+            for c in range(NC):
+                cols = slice(c * BANK, (c + 1) * BANK)
+                nc.gpsimd.tensor_tensor(
+                    out=rb_of[i][:, cols], in0=r_sb[:, i, cols], in1=bias_bc[:, cols], op=ALU.add
                 )
 
-        def add_residual(g, c):
-            if c == 0:
-                y_of[g] = rows.tile([P, TG, D], F32, name="y")
-                sums_of[g] = small.tile([P, TG, NC], F32, name="chunk_sums")
+        def multiply(i, c):
+            toks = slice(i * P, (i + 1) * P)
             cols = slice(c * BANK, (c + 1) * BANK)
-            for i in range(TG):
-                zbt = psum_t.tile([P, BANK], F32, name="zbt", tag="tok")
-                for jj in range(F_PER_CHUNK):
-                    nc.tensor.transpose(zbt[:, jj * P : (jj + 1) * P], zb_of[g, c][:, jj, i * P : (i + 1) * P], ident_f[:])
-                nc.vector.scalar_tensor_tensor(
-                    out=y_of[g][:, i, cols],
-                    in0=zbt[:],
-                    scalar=0.0,
-                    in1=r_sb[:, g * TG + i, cols],
-                    op0=ALU.add,
-                    op1=ALU.add,
-                    accum_out=sums_of[g][:, i, c : c + 1],
-                )
-            if c == NC - 1:
-                row_sum = small.tile([P, TG], F32, name="row_sum")
-                nc.vector.tensor_reduce(out=row_sum[:], in_=sums_of[g][:], axis=AX.X, op=ALU.add)
-                neg_mean_of[g] = small.tile([P, TG], F32, name="neg_mean")
-                nc.vector.tensor_scalar_mul(out=neg_mean_of[g][:], in0=row_sum[:], scalar1=-1.0 / D)
+            z_of[i, c] = psum_z.tile([P, BANK], F32, name="z", tag="z")
+            nc.tensor.matmul_mx(
+                out=z_of[i, c][:],
+                lhsT=x_codes[:, toks].bitcast(FP8X4),
+                lhsT_scale=x_scales[:, toks],
+                rhs=w_codes[:, cols].bitcast(FP8X4),
+                rhs_scale=w_scales[:, cols],
+                start=True,
+                stop=True,
+            )
 
-        def normalise(g, i):
-            neg_mean = neg_mean_of[g][:, i : i + 1]
+        def add(i, c):
+            if c == 0:
+                y_of[i] = work.tile([P, D], F32, name="y")
+                sums_of[i] = small.tile([P, NC], F32, name="sums")
+            cols = slice(c * BANK, (c + 1) * BANK)
+            nc.vector.scalar_tensor_tensor(
+                out=y_of[i][:, cols],
+                in0=z_of[i, c][:],
+                scalar=0.0,
+                in1=rb_of[i][:, cols],
+                op0=ALU.add,
+                op1=ALU.add,
+                accum_out=sums_of[i][:, c : c + 1],
+            )
+
+        def statistics(i):
+            neg_mean_of[i] = small.tile([P, 1], F32, name="neg_mean")
+            parts = small.tile([P, NC], F32, name="parts")
+            nc.scalar.activation(
+                out=parts[:], in_=sums_of[i][:], func=ACT.Copy, scale=-1.0 / D, accum_out=neg_mean_of[i][:]
+            )
             squares = work.tile([P, D], BF16, name="squares")
             sq_sum = small.tile([P, 1], F32, name="sq_sum")
             nc.scalar.activation(
-                out=squares[:], in_=y_of[g][:, i, :], func=ACT.Square, bias=neg_mean, scale=1.0, accum_out=sq_sum[:]
+                out=squares[:], in_=y_of[i][:], func=ACT.Square, bias=neg_mean_of[i][:], scale=1.0, accum_out=sq_sum[:]
             )
-            std = small.tile([P, 1], F32, name="std")
-            nc.scalar.activation(out=std[:], in_=sq_sum[:], func=ACT.Sqrt, bias=eps[:], scale=1.0 / D)
-            o = work.tile([P, D], F32, name="o")
-            nc.vector.scalar_tensor_tensor(
-                out=o[:], in0=y_of[g][:, i, :], scalar=neg_mean, in1=gain_bc[:], op0=ALU.add, op1=ALU.mult
-            )
-            rstd = small.tile([P, 1], F32, name="rstd")
-            nc.vector.reciprocal(out=rstd[:], in_=std[:])
-            nc.vector.scalar_tensor_tensor(
-                out=o[:], in0=o[:], scalar=rstd[:], in1=shift_bc[:], op0=ALU.mult, op1=ALU.add
-            )
-            nc.sync.dma_start(out=out_view[:, g * TG + i, :], in_=o[:])
+            std_of[i] = small.tile([P, 1], F32, name="std")
+            nc.scalar.activation(out=std_of[i][:], in_=sq_sum[:], func=ACT.Sqrt, bias=eps[:], scale=1.0 / D)
 
-        quantise_x(0)
-        bias_ps = psum_t.tile([P, P], BF16, tag="tok")
-        nc.tensor.transpose(bias_ps[:], bias_rows[:], ident_b[:])
-        nc.vector.tensor_copy(out=bias_col[:], in_=bias_ps[:, 0:NF])
-        quantise_w(0)
+        def invert(i):
+            rstd_of[i] = small.tile([P, 1], F32, name="rstd")
+            nc.vector.reciprocal(out=rstd_of[i][:], in_=std_of[i][:])
+
+        def centre(i, c):
+            centred_of[i, c] = psum_c.tile([P, F_PER_CHUNK, P], F32, name="centred", tag="c")
+            for jj in range(F_PER_CHUNK):
+                j = c * F_PER_CHUNK + jj
+                nc.tensor.matmul(
+                    out=centred_of[i, c][:, jj, :],
+                    lhsT=y_of[i][:, j * P : (j + 1) * P],
+                    rhs=ident_f[:],
+                    start=True,
+                    stop=False,
+                    is_transpose=True,
+                )
+                nc.tensor.matmul(
+                    out=centred_of[i, c][:, jj, :],
+                    lhsT=neg_mean_of[i][:].to_broadcast([P, P]),
+                    rhs=ident_f[:],
+                    start=False,
+                    stop=True,
+                    is_transpose=True,
+                )
+
+        def scale(i, c):
+            scaled_of[i, c] = cols_pool.tile([P, F_PER_CHUNK, P], F32, name="scaled")
+            for jj in range(F_PER_CHUNK):
+                j = NF + c * F_PER_CHUNK + jj
+                nc.scalar.activation(
+                    out=scaled_of[i, c][:, jj, :], in_=centred_of[i, c][:, jj, :], func=ACT.Copy, scale=vec_col[:, j : j + 1]
+                )
+
+        def turn_back(i, c):
+            back_of[i, c] = psum_o.tile([P, BANK], F32, name="back", tag="o")
+            for jj in range(F_PER_CHUNK):
+                nc.tensor.transpose(back_of[i, c][:, jj * P : (jj + 1) * P], scaled_of[i, c][:, jj, :], ident_f[:])
+
+        def finish(i, c):
+            if c == 0:
+                o_of[i] = work.tile([P, D], F32, name="o")
+            cols = slice(c * BANK, (c + 1) * BANK)
+            nc.vector.scalar_tensor_tensor(
+                out=o_of[i][:, cols],
+                in0=back_of[i, c][:],
+                scalar=rstd_of[i][:],
+                in1=shift_bc[:, cols],
+                op0=ALU.mult,
+                op1=ALU.add,
+            )
+            if c == NC - 1:
+                nc.sync.dma_start(out=out_view[:, i, :], in_=o_of[i][:])
+
+        ctx.enter_context(tc.manual_schedule())
+        turn_vectors()
+        spread_bias(0)
+        spread_bias(1)
+        w_group(0, nc.vector.tensor_copy)
+        x_order(0)
+        x_order(1)
+        x_turn(0)
+        spread_bias(2)
+        spread_bias(3)
+        residual_and_bias(0)
+        w_quantise(0)
+        x_quantise(0)
         multiply(0, 0)
-        for g in range(NG + 1):
-            for c in range(NC):
-                if g == 0 and c + 1 < NC:
-                    quantise_w(c + 1)
-                if g + 1 < NG and c == 0:
-                    quantise_x(g + 1)
-                if c + 1 < NC and g < NG:
-                    multiply(g, c + 1)
-                if c + 1 == NC and g + 1 < NG:
-                    multiply(g + 1, 0)
-                if g < NG:
-                    add_residual(g, c)
-                if g >= 1:
-                    normalise(g - 1, c)
+        w_group(1, nc.vector.tensor_copy)
+        w_group(2, nc.scalar.copy)
+        w_quantise(1)
+        multiply(0, 1)
+        add(0, 0)
+        w_group(3, nc.scalar.copy)
+        w_quantise(2)
+        multiply(0, 2)
+        add(0, 1)
+        x_order(2)
+        x_order(3)
+        x_turn(2)
+        add(0, 2)
+        w_quantise(3)
+        multiply(0, 3)
+        add(0, 3)
+
+        for s in range(NT):
+            if s + 1 < NT:
+                residual_and_bias(s + 1)
+            statistics(s)
+            centre(s, 0)
+            if s % 2 == 0 and s + 2 < NT:
+                x_quantise(s + 2)
+            if s >= 1:
+                invert(s - 1)
+                finish(s - 1, 0)
+                turn_back(s - 1, 2)
+                finish(s - 1, 1)
+            centre(s, 1)
+            if s >= 1:
+                turn_back(s - 1, 3)
+                finish(s - 1, 2)
+                finish(s - 1, 3)
+            if s + 1 < NT:
+                for c in range(NC):
+                    multiply(s + 1, c)
+            scale(s, 0)
+            centre(s, 2)
+            scale(s, 1)
+            centre(s, 3)
+            scale(s, 2)
+            turn_back(s, 0)
+            scale(s, 3)
+            turn_back(s, 1)
+            if (s + 1) % 2 == 0 and s + 3 < NT:
+                x_order(s + 3)
+                x_order(s + 4)
+                x_turn(s + 3)
+            if s + 1 < NT:
+                for c in range(NC):
+                    add(s + 1, c)
+        invert(NT - 1)
+        finish(NT - 1, 0)
+        turn_back(NT - 1, 2)
+        finish(NT - 1, 1)
+        turn_back(NT - 1, 3)
+        finish(NT - 1, 2)
+        finish(NT - 1, 3)

@@ -22,6 +22,7 @@ BANK = 512
 NC = D // BANK
 F_PER_CHUNK = BANK // P
 LN_EPS = 1e-5
+REPEATS = (3, 2)
 
 FLOPS = 2 * LQ * H * DV * D
 
@@ -33,6 +34,7 @@ def tile_multiheadattention_pb_kernel(tc, attn_out, residual, proj_w, proj_b, ln
         x_pool = ctx.enter_context(tc.tile_pool(name="x_pool", bufs=NT // 2))
         work = ctx.enter_context(tc.tile_pool(name="work", bufs=3))
         cols_pool = ctx.enter_context(tc.tile_pool(name="cols_pool", bufs=8))
+        pairs = ctx.enter_context(tc.tile_pool(name="pairs", bufs=2))
         small = ctx.enter_context(tc.tile_pool(name="small", bufs=4))
         psum_z = ctx.enter_context(tc.psum_pool(name="psum_z", bufs=4))
         psum_c = ctx.enter_context(tc.psum_pool(name="psum_c", bufs=2))
@@ -155,6 +157,7 @@ def tile_multiheadattention_pb_kernel(tc, attn_out, residual, proj_w, proj_b, ln
         neg_mean_of = {}
         std_of = {}
         centred_of = {}
+        turned_of = {}
         scaled_of = {}
         rstd_of = {}
         back_of = {}
@@ -172,19 +175,20 @@ def tile_multiheadattention_pb_kernel(tc, attn_out, residual, proj_w, proj_b, ln
             toks = slice(i * P, (i + 1) * P)
             cols = slice(c * BANK, (c + 1) * BANK)
             z_of[i, c] = psum_z.tile([P, BANK], F32, name="z", tag="z")
-            nc.tensor.matmul_mx(
-                out=z_of[i, c][:],
-                lhsT=x_codes[:, toks].bitcast(FP8X4),
-                lhsT_scale=x_scales[:, toks],
-                rhs=w_codes[:, cols].bitcast(FP8X4),
-                rhs_scale=w_scales[:, cols],
-                start=True,
-                stop=True,
-            )
+            for again in range(REPEATS[min(i, 1)]):
+                nc.tensor.matmul_mx(
+                    out=z_of[i, c][:],
+                    lhsT=x_codes[:, toks].bitcast(FP8X4),
+                    lhsT_scale=x_scales[:, toks],
+                    rhs=w_codes[:, cols].bitcast(FP8X4),
+                    rhs_scale=w_scales[:, cols],
+                    start=True,
+                    stop=True,
+                )
 
         def add(i, c):
             if c == 0:
-                y_of[i] = work.tile([P, D], F32, name="y")
+                y_of[i] = pairs.tile([P, D], F32, name="y")
                 sums_of[i] = small.tile([P, NC], F32, name="sums")
             cols = slice(c * BANK, (c + 1) * BANK)
             nc.vector.scalar_tensor_tensor(
@@ -203,7 +207,7 @@ def tile_multiheadattention_pb_kernel(tc, attn_out, residual, proj_w, proj_b, ln
             nc.scalar.activation(
                 out=parts[:], in_=sums_of[i][:], func=ACT.Copy, scale=-1.0 / D, accum_out=neg_mean_of[i][:]
             )
-            squares = work.tile([P, D], BF16, name="squares")
+            squares = pairs.tile([P, D], BF16, name="squares")
             sq_sum = small.tile([P, 1], F32, name="sq_sum")
             nc.scalar.activation(
                 out=squares[:], in_=y_of[i][:], func=ACT.Square, bias=neg_mean_of[i][:], scale=1.0, accum_out=sq_sum[:]
@@ -215,33 +219,24 @@ def tile_multiheadattention_pb_kernel(tc, attn_out, residual, proj_w, proj_b, ln
             rstd_of[i] = small.tile([P, 1], F32, name="rstd")
             nc.vector.reciprocal(out=rstd_of[i][:], in_=std_of[i][:])
 
-        def centre(i, c):
-            centred_of[i, c] = psum_c.tile([P, F_PER_CHUNK, P], F32, name="centred", tag="c")
+        def centre(i):
+            centred_of[i] = pairs.tile([P, D], F32, name="centred")
+            nc.vector.tensor_scalar(
+                out=centred_of[i][:], in0=y_of[i][:], scalar1=neg_mean_of[i][:], scalar2=None, op0=ALU.add
+            )
+
+        def turn(i, c):
+            turned_of[i, c] = psum_c.tile([P, F_PER_CHUNK, P], F32, name="turned", tag="c")
             for jj in range(F_PER_CHUNK):
                 j = c * F_PER_CHUNK + jj
-                nc.tensor.matmul(
-                    out=centred_of[i, c][:, jj, :],
-                    lhsT=y_of[i][:, j * P : (j + 1) * P],
-                    rhs=ident_f[:],
-                    start=True,
-                    stop=False,
-                    is_transpose=True,
-                )
-                nc.tensor.matmul(
-                    out=centred_of[i, c][:, jj, :],
-                    lhsT=neg_mean_of[i][:].to_broadcast([P, P]),
-                    rhs=ident_f[:],
-                    start=False,
-                    stop=True,
-                    is_transpose=True,
-                )
+                nc.tensor.transpose(turned_of[i, c][:, jj, :], centred_of[i][:, j * P : (j + 1) * P], ident_f[:])
 
         def scale(i, c):
             scaled_of[i, c] = cols_pool.tile([P, F_PER_CHUNK, P], F32, name="scaled")
             for jj in range(F_PER_CHUNK):
                 j = NF + c * F_PER_CHUNK + jj
                 nc.scalar.activation(
-                    out=scaled_of[i, c][:, jj, :], in_=centred_of[i, c][:, jj, :], func=ACT.Copy, scale=vec_col[:, j : j + 1]
+                    out=scaled_of[i, c][:, jj, :], in_=turned_of[i, c][:, jj, :], func=ACT.Copy, scale=vec_col[:, j : j + 1]
                 )
 
         def turn_back(i, c):
@@ -299,33 +294,38 @@ def tile_multiheadattention_pb_kernel(tc, attn_out, residual, proj_w, proj_b, ln
             if s + 1 < NT:
                 residual_and_bias(s + 1)
             statistics(s)
-            centre(s, 0)
-            if s % 2 == 0 and s + 2 < NT:
-                x_quantise(s + 2)
+            if s + 1 < NT:
+                multiply(s + 1, 0)
+                multiply(s + 1, 1)
             if s >= 1:
                 invert(s - 1)
                 finish(s - 1, 0)
                 turn_back(s - 1, 2)
                 finish(s - 1, 1)
-            centre(s, 1)
-            if s >= 1:
                 turn_back(s - 1, 3)
+            centre(s)
+            if s % 2 == 0 and s + 2 < NT:
+                x_quantise(s + 2)
+            turn(s, 0)
+            turn(s, 1)
+            if s >= 1:
                 finish(s - 1, 2)
                 finish(s - 1, 3)
-            if s + 1 < NT:
-                for c in range(NC):
-                    multiply(s + 1, c)
+            if (s + 1) % 2 == 0 and s + 3 < NT:
+                x_order(s + 3)
+                x_order(s + 4)
             scale(s, 0)
-            centre(s, 2)
+            if s + 1 < NT:
+                multiply(s + 1, 2)
+                multiply(s + 1, 3)
+            turn(s, 2)
             scale(s, 1)
-            centre(s, 3)
+            turn(s, 3)
             scale(s, 2)
             turn_back(s, 0)
             scale(s, 3)
             turn_back(s, 1)
             if (s + 1) % 2 == 0 and s + 3 < NT:
-                x_order(s + 3)
-                x_order(s + 4)
                 x_turn(s + 3)
             if s + 1 < NT:
                 for c in range(NC):

@@ -22,7 +22,7 @@ BANK = 512
 NC = D // BANK
 F_PER_CHUNK = BANK // P
 LN_EPS = 1e-5
-REPEATS = (3, 2)
+REPEATS = (3, 1)
 
 FLOPS = 2 * LQ * H * DV * D
 
@@ -225,8 +225,13 @@ def tile_multiheadattention_pb_kernel(tc, attn_out, residual, proj_w, proj_b, ln
                 out=centred_of[i][:], in0=y_of[i][:], scalar1=neg_mean_of[i][:], scalar2=None, op0=ALU.add
             )
 
+        def keep_clock(bank):
+            nc.tensor.matmul(out=bank, lhsT=ident_f[:], rhs=ident_f[:], start=True, stop=True)
+
         def turn(i, c):
             turned_of[i, c] = psum_c.tile([P, F_PER_CHUNK, P], F32, name="turned", tag="c")
+            if c % 2 == 0:
+                keep_clock(turned_of[i, c][:, 0, :])
             for jj in range(F_PER_CHUNK):
                 j = c * F_PER_CHUNK + jj
                 nc.tensor.transpose(turned_of[i, c][:, jj, :], centred_of[i][:, j * P : (j + 1) * P], ident_f[:])
@@ -241,6 +246,8 @@ def tile_multiheadattention_pb_kernel(tc, attn_out, residual, proj_w, proj_b, ln
 
         def turn_back(i, c):
             back_of[i, c] = psum_o.tile([P, BANK], F32, name="back", tag="o")
+            if c % 2 == 0:
+                keep_clock(back_of[i, c][:, 0:P])
             for jj in range(F_PER_CHUNK):
                 nc.tensor.transpose(back_of[i, c][:, jj * P : (jj + 1) * P], scaled_of[i, c][:, jj, :], ident_f[:])
 

@@ -22,7 +22,9 @@ BANK = 512
 NC = D // BANK
 F_PER_CHUNK = BANK // P
 LN_EPS = 1e-5
-REPEATS = (3, 1)
+CHUNK_ORDER = (2, 3, 0, 1)
+VECTOR_SCALES = (2, 3)
+REPEATS = (1, 1)
 
 FLOPS = 2 * LQ * H * DV * D
 
@@ -40,10 +42,10 @@ def tile_multiheadattention_pb_kernel(tc, attn_out, residual, proj_w, proj_b, ln
         psum_c = ctx.enter_context(tc.psum_pool(name="psum_c", bufs=2))
         psum_o = ctx.enter_context(tc.psum_pool(name="psum_o", bufs=2))
 
-        vec_rows = keep.tile([P, P], BF16)
-        nc.vector.memset(vec_rows[:], 0.0)
-        nc.sync.dma_start(out=vec_rows[0:NF, :], in_=proj_b.rearrange("(j q) -> j q", q=P))
-        nc.sync.dma_start(out=vec_rows[NF : 2 * NF, :], in_=ln_g.rearrange("(j q) -> j q", q=P))
+        gain_rows = keep.tile([P, P], BF16)
+        nc.vector.memset(gain_rows[:], 0.0)
+        nc.sync.dma_start(out=gain_rows[0:NF, :], in_=ln_g.rearrange("(j q) -> j q", q=P))
+        bias_bc = keep.tile([P, D], BF16)
         x_raw = {}
         x_view = attn_out.rearrange("h (p t) j -> p h t j", t=NT)
         w_raw = keep.tile([P, H, D], BF16)
@@ -51,6 +53,7 @@ def tile_multiheadattention_pb_kernel(tc, attn_out, residual, proj_w, proj_b, ln
         r_sb = keep.tile([P, NT, D], BF16)
         r_view = residual.rearrange("(p t) n -> p t n", t=NT)
         shift_bc = keep.tile([P, D], BF16)
+        gain_bc = keep.tile([P, D], BF16)
 
         def load_x(t0):
             x_raw[t0] = x_pool.tile([P, H, 2, DV], BF16, name="x_pair")
@@ -66,20 +69,23 @@ def tile_multiheadattention_pb_kernel(tc, attn_out, residual, proj_w, proj_b, ln
         def load_r(t):
             nc.sync.dma_start(out=r_sb[:, t, :], in_=r_view[:, t, :])
 
-        load_w(0)
         load_x(0)
+        load_w(0)
         load_w(1)
         load_w(2)
-        load_r(0)
         load_w(3)
+        load_r(0)
+        nc.sync.dma_start(out=bias_bc[:], in_=proj_b.partition_broadcast(P))
         load_x(2)
-        load_r(1)
         load_x(4)
-        load_r(2)
         load_x(6)
+        load_r(1)
+        load_r(2)
         nc.sync.dma_start(out=shift_bc[:], in_=ln_b.partition_broadcast(P))
         for t in range(3, NT):
             load_r(t)
+
+        nc.sync.dma_start(out=gain_bc[:], in_=ln_g.partition_broadcast(P))
 
         eps = keep.tile([P, 1], F32)
         nc.vector.memset(eps[:], LN_EPS)
@@ -97,12 +103,11 @@ def tile_multiheadattention_pb_kernel(tc, attn_out, residual, proj_w, proj_b, ln
         w_grouped = keep.tile([P, D, H], BF16, align_bytes=64)
         w_codes = keep.tile([P, D], U32, align_bytes=64)
         w_scales = keep.tile([P, D], U8, align_bytes=64)
-        vec_col = keep.tile([P, 2 * NF], F32)
-        bias_bc = keep.tile([P, D], BF16)
+        gain_col = keep.tile([P, NF], F32)
         out_view = out.rearrange("(p t) n -> p t n", t=NT)
 
-        def x_order(t):
-            nc.vector.tensor_copy(
+        def x_order(t, copy):
+            copy(
                 out=x_words[:, t, :, :].rearrange("p u (h a) -> p u h a", h=H),
                 in_=x_raw[t - t % 2][:, :, t % 2, :].bitcast(F32).rearrange("p h (a u) -> p u h a", u=2),
             )
@@ -124,8 +129,8 @@ def tile_multiheadattention_pb_kernel(tc, attn_out, residual, proj_w, proj_b, ln
             toks = slice(t0 * P, (t0 + 2) * P)
             nc.vector.quantize_mx(out=x_codes[:, toks].bitcast(FP8X4), scales=x_scales[:, toks], in_=x_grouped_pair(t0))
 
-        def w_group(c, copy):
-            cols = slice(c * BANK, (c + 1) * BANK)
+        def w_group(c, copy, first=0, last=BANK):
+            cols = slice(c * BANK + first, c * BANK + last)
             copy(out=w_grouped[:, cols, :], in_=w_raw[:, :, cols].rearrange("q i n -> q n i"))
 
         def w_quantise(c):
@@ -136,19 +141,10 @@ def tile_multiheadattention_pb_kernel(tc, attn_out, residual, proj_w, proj_b, ln
                 in_=w_grouped[:, cols, :].rearrange("q n i -> q (n i)"),
             )
 
-        def turn_vectors():
+        def turn_gain():
             rows_ps = psum_o.tile([P, P], BF16, name="rows_ps", tag="o")
-            nc.tensor.transpose(rows_ps[:], vec_rows[:], ident_b[:])
-            nc.vector.tensor_copy(out=vec_col[:], in_=rows_ps[:, 0 : 2 * NF])
-
-        def spread_bias(c):
-            spread = psum_z.tile([P, BANK], F32, name="spread", tag="z")
-            for jj in range(F_PER_CHUNK):
-                j = c * F_PER_CHUNK + jj
-                nc.tensor.transpose(
-                    spread[:, jj * P : (jj + 1) * P], vec_col[:, j : j + 1].to_broadcast([P, P]), ident_f[:]
-                )
-            nc.scalar.copy(out=bias_bc[:, c * BANK : (c + 1) * BANK], in_=spread[:])
+            nc.tensor.transpose(rows_ps[:], gain_rows[:], ident_b[:])
+            nc.vector.tensor_copy(out=gain_col[:], in_=rows_ps[:, 0:NF])
 
         rb_of = {}
         y_of = {}
@@ -163,11 +159,12 @@ def tile_multiheadattention_pb_kernel(tc, attn_out, residual, proj_w, proj_b, ln
         back_of = {}
         o_of = {}
 
-        def residual_and_bias(i):
-            rb_of[i] = work.tile([P, D], F32, name="rb")
-            for c in range(NC):
+        def residual_and_bias(i, engine, chunks=range(NC)):
+            if i not in rb_of:
+                rb_of[i] = work.tile([P, D], F32, name="rb")
+            for c in chunks:
                 cols = slice(c * BANK, (c + 1) * BANK)
-                nc.gpsimd.tensor_tensor(
+                engine.tensor_tensor(
                     out=rb_of[i][:, cols], in0=r_sb[:, i, cols], in1=bias_bc[:, cols], op=ALU.add
                 )
 
@@ -201,12 +198,22 @@ def tile_multiheadattention_pb_kernel(tc, attn_out, residual, proj_w, proj_b, ln
                 accum_out=sums_of[i][:, c : c + 1],
             )
 
-        def statistics(i):
-            neg_mean_of[i] = small.tile([P, 1], F32, name="neg_mean")
+        def centre(i):
+            neg_mean = neg_mean_of[i] = small.tile([P, 1], F32, name="neg_mean")
             parts = small.tile([P, NC], F32, name="parts")
             nc.scalar.activation(
-                out=parts[:], in_=sums_of[i][:], func=ACT.Copy, scale=-1.0 / D, accum_out=neg_mean_of[i][:]
+                out=parts[:], in_=sums_of[i][:], func=ACT.Copy, scale=-1.0 / D, accum_out=neg_mean[:]
             )
+            if i == NT - 1:
+                return
+            centred_of[i] = pairs.tile([P, D], F32, name="centred")
+            for c in CHUNK_ORDER:
+                cols = slice(c * BANK, (c + 1) * BANK)
+                nc.scalar.activation(
+                    out=centred_of[i][:, cols], in_=y_of[i][:, cols], func=ACT.Identity, bias=neg_mean[:], scale=1.0
+                )
+
+        def deviation(i):
             squares = pairs.tile([P, D], BF16, name="squares")
             sq_sum = small.tile([P, 1], F32, name="sq_sum")
             nc.scalar.activation(
@@ -219,18 +226,12 @@ def tile_multiheadattention_pb_kernel(tc, attn_out, residual, proj_w, proj_b, ln
             rstd_of[i] = small.tile([P, 1], F32, name="rstd")
             nc.vector.reciprocal(out=rstd_of[i][:], in_=std_of[i][:])
 
-        def centre(i):
-            centred_of[i] = pairs.tile([P, D], F32, name="centred")
-            nc.vector.tensor_scalar(
-                out=centred_of[i][:], in0=y_of[i][:], scalar1=neg_mean_of[i][:], scalar2=None, op0=ALU.add
-            )
-
         def keep_clock(bank):
             nc.tensor.matmul(out=bank, lhsT=ident_f[:], rhs=ident_f[:], start=True, stop=True)
 
-        def turn(i, c):
+        def turn(i, c, warm=False):
             turned_of[i, c] = psum_c.tile([P, F_PER_CHUNK, P], F32, name="turned", tag="c")
-            if c % 2 == 0:
+            if warm:
                 keep_clock(turned_of[i, c][:, 0, :])
             for jj in range(F_PER_CHUNK):
                 j = c * F_PER_CHUNK + jj
@@ -238,21 +239,48 @@ def tile_multiheadattention_pb_kernel(tc, attn_out, residual, proj_w, proj_b, ln
 
         def scale(i, c):
             scaled_of[i, c] = cols_pool.tile([P, F_PER_CHUNK, P], F32, name="scaled")
+            if c in VECTOR_SCALES:
+                gains = gain_col[:, c * F_PER_CHUNK : (c + 1) * F_PER_CHUNK]
+                nc.vector.tensor_tensor(
+                    out=scaled_of[i, c][:],
+                    in0=turned_of[i, c][:],
+                    in1=gains.unsqueeze(2).to_broadcast([P, F_PER_CHUNK, P]),
+                    op=ALU.mult,
+                )
+                return
             for jj in range(F_PER_CHUNK):
-                j = NF + c * F_PER_CHUNK + jj
+                j = c * F_PER_CHUNK + jj
                 nc.scalar.activation(
-                    out=scaled_of[i, c][:, jj, :], in_=turned_of[i, c][:, jj, :], func=ACT.Copy, scale=vec_col[:, j : j + 1]
+                    out=scaled_of[i, c][:, jj, :], in_=turned_of[i, c][:, jj, :], func=ACT.Copy, scale=gain_col[:, j : j + 1]
                 )
 
-        def turn_back(i, c):
+        def turn_back(i, c, warm=False):
             back_of[i, c] = psum_o.tile([P, BANK], F32, name="back", tag="o")
-            if c % 2 == 0:
+            if warm:
                 keep_clock(back_of[i, c][:, 0:P])
             for jj in range(F_PER_CHUNK):
                 nc.tensor.transpose(back_of[i, c][:, jj * P : (jj + 1) * P], scaled_of[i, c][:, jj, :], ident_f[:])
 
+        def scale_last(i):
+            o_of[i] = work.tile([P, D], F32, name="o")
+            nc.vector.scalar_tensor_tensor(
+                out=o_of[i][:], in0=y_of[i][:], scalar=neg_mean_of[i][:], in1=gain_bc[:], op0=ALU.add, op1=ALU.mult
+            )
+
+        def finish_last(i, c):
+            cols = slice(c * BANK, (c + 1) * BANK)
+            nc.vector.scalar_tensor_tensor(
+                out=o_of[i][:, cols],
+                in0=o_of[i][:, cols],
+                scalar=rstd_of[i][:],
+                in1=shift_bc[:, cols],
+                op0=ALU.mult,
+                op1=ALU.add,
+            )
+            nc.sync.dma_start(out=out_view[:, i, cols], in_=o_of[i][:, cols])
+
         def finish(i, c):
-            if c == 0:
+            if c == CHUNK_ORDER[0]:
                 o_of[i] = work.tile([P, D], F32, name="o")
             cols = slice(c * BANK, (c + 1) * BANK)
             nc.vector.scalar_tensor_tensor(
@@ -263,84 +291,92 @@ def tile_multiheadattention_pb_kernel(tc, attn_out, residual, proj_w, proj_b, ln
                 op0=ALU.mult,
                 op1=ALU.add,
             )
-            if c == NC - 1:
+            if c == CHUNK_ORDER[-1]:
                 nc.sync.dma_start(out=out_view[:, i, :], in_=o_of[i][:])
 
         ctx.enter_context(tc.manual_schedule())
-        turn_vectors()
-        spread_bias(0)
-        spread_bias(1)
-        w_group(0, nc.vector.tensor_copy)
-        x_order(0)
-        x_order(1)
+        turn_gain()
+        x_order(0, nc.vector.tensor_copy)
+        x_order(1, nc.vector.tensor_copy)
         x_turn(0)
-        spread_bias(2)
-        spread_bias(3)
-        residual_and_bias(0)
+        w_group(0, nc.vector.tensor_copy)
         w_quantise(0)
+        w_group(1, nc.scalar.copy)
         x_quantise(0)
         multiply(0, 0)
-        w_group(1, nc.vector.tensor_copy)
-        w_group(2, nc.scalar.copy)
-        w_quantise(1)
-        multiply(0, 1)
-        add(0, 0)
-        w_group(3, nc.scalar.copy)
+        w_group(2, nc.vector.tensor_copy)
         w_quantise(2)
         multiply(0, 2)
-        add(0, 1)
-        x_order(2)
-        x_order(3)
-        x_turn(2)
-        add(0, 2)
+        w_group(3, nc.vector.tensor_copy, 0, 256)
+        w_group(3, nc.scalar.copy, 256, BANK)
+        w_quantise(1)
+        multiply(0, 1)
         w_quantise(3)
         multiply(0, 3)
+        for t in range(2, NT):
+            x_order(t, nc.scalar.copy)
+        x_turn(2)
+        x_turn(4)
+        x_turn(6)
+        residual_and_bias(0, nc.vector)
+        add(0, 0)
+        add(0, 2)
+        add(0, 1)
         add(0, 3)
+        x_quantise(2)
+        multiply(1, 0)
+        multiply(1, 1)
+        multiply(1, 2)
+        multiply(1, 3)
+        residual_and_bias(1, nc.gpsimd)
 
-        for s in range(NT):
+        for s in range(1, NT + 1):
             if s + 1 < NT:
-                residual_and_bias(s + 1)
-            statistics(s)
+                residual_and_bias(s + 1, nc.gpsimd)
+            centre(s - 1)
+            deviation(s - 1)
+            if s == 1:
+                x_quantise(4)
+            if s == 2:
+                x_quantise(6)
+            if s >= 2:
+                invert(s - 2)
+                finish(s - 2, 2)
+                turn_back(s - 2, 0, warm=True)
+            if s < NT:
+                add(s, 0)
+                turn(s - 1, 2)
+            if s >= 2:
+                finish(s - 2, 3)
+                turn_back(s - 2, 1)
+            if s < NT:
+                add(s, 1)
+                turn(s - 1, 3)
+            else:
+                scale_last(s - 1)
             if s + 1 < NT:
                 multiply(s + 1, 0)
                 multiply(s + 1, 1)
-            if s >= 1:
-                invert(s - 1)
-                finish(s - 1, 0)
-                turn_back(s - 1, 2)
-                finish(s - 1, 1)
+            if s < NT:
+                scale(s - 1, 2)
+            if s >= 2:
+                finish(s - 2, 0)
+            if s < NT:
+                add(s, 2)
+                turn(s - 1, 0, warm=True)
+                scale(s - 1, 3)
+                turn(s - 1, 1)
+            if s >= 2:
+                finish(s - 2, 1)
+            if s < NT:
+                add(s, 3)
+                turn_back(s - 1, 2, warm=True)
                 turn_back(s - 1, 3)
-            centre(s)
-            if s % 2 == 0 and s + 2 < NT:
-                x_quantise(s + 2)
-            turn(s, 0)
-            turn(s, 1)
-            if s >= 1:
-                finish(s - 1, 2)
-                finish(s - 1, 3)
-            if (s + 1) % 2 == 0 and s + 3 < NT:
-                x_order(s + 3)
-                x_order(s + 4)
-            scale(s, 0)
+                scale(s - 1, 0)
+                scale(s - 1, 1)
             if s + 1 < NT:
                 multiply(s + 1, 2)
                 multiply(s + 1, 3)
-            turn(s, 2)
-            scale(s, 1)
-            turn(s, 3)
-            scale(s, 2)
-            turn_back(s, 0)
-            scale(s, 3)
-            turn_back(s, 1)
-            if (s + 1) % 2 == 0 and s + 3 < NT:
-                x_turn(s + 3)
-            if s + 1 < NT:
-                for c in range(NC):
-                    add(s + 1, c)
         invert(NT - 1)
-        finish(NT - 1, 0)
-        turn_back(NT - 1, 2)
-        finish(NT - 1, 1)
-        turn_back(NT - 1, 3)
-        finish(NT - 1, 2)
-        finish(NT - 1, 3)
+        for c in range(NC):
+            finish_last(NT - 1, c)

@@ -23,7 +23,8 @@ NC = D // BANK
 F_PER_CHUNK = BANK // P
 LN_EPS = 1e-5
 CHUNK_ORDER = (2, 3, 0, 1)
-VECTOR_SCALES = (2, 3)
+SCALAR_CENTRES = (3, 0, 1)
+TURNED_LAST = (0,)
 REPEATS = (1, 1)
 
 FLOPS = 2 * LQ * H * DV * D
@@ -34,6 +35,7 @@ def tile_multiheadattention_pb_kernel(tc, attn_out, residual, proj_w, proj_b, ln
     with ExitStack() as ctx:
         keep = ctx.enter_context(tc.tile_pool(name="keep", bufs=1))
         x_pool = ctx.enter_context(tc.tile_pool(name="x_pool", bufs=NT // 2))
+        w_pool = ctx.enter_context(tc.tile_pool(name="w_pool", bufs=NC))
         work = ctx.enter_context(tc.tile_pool(name="work", bufs=3))
         cols_pool = ctx.enter_context(tc.tile_pool(name="cols_pool", bufs=8))
         pairs = ctx.enter_context(tc.tile_pool(name="pairs", bufs=2))
@@ -42,13 +44,14 @@ def tile_multiheadattention_pb_kernel(tc, attn_out, residual, proj_w, proj_b, ln
         psum_c = ctx.enter_context(tc.psum_pool(name="psum_c", bufs=2))
         psum_o = ctx.enter_context(tc.psum_pool(name="psum_o", bufs=2))
 
-        gain_rows = keep.tile([P, P], BF16)
-        nc.vector.memset(gain_rows[:], 0.0)
-        nc.sync.dma_start(out=gain_rows[0:NF, :], in_=ln_g.rearrange("(j q) -> j q", q=P))
+        vec_rows = keep.tile([P, P], BF16)
+        nc.vector.memset(vec_rows[:], 0.0)
+        nc.sync.dma_start(out=vec_rows[0:NF, :], in_=proj_b.rearrange("(j q) -> j q", q=P))
+        nc.sync.dma_start(out=vec_rows[NF : 2 * NF, :], in_=ln_g.rearrange("(j q) -> j q", q=P))
         bias_bc = keep.tile([P, D], BF16)
         x_raw = {}
         x_view = attn_out.rearrange("h (p t) j -> p h t j", t=NT)
-        w_raw = keep.tile([P, H, D], BF16)
+        w_raw = {}
         w_view = proj_w.rearrange("(q i) n -> q i n", i=H)
         r_sb = keep.tile([P, NT, D], BF16)
         r_view = residual.rearrange("(p t) n -> p t n", t=NT)
@@ -64,7 +67,8 @@ def tile_multiheadattention_pb_kernel(tc, attn_out, residual, proj_w, proj_b, ln
 
         def load_w(c):
             cols = slice(c * BANK, (c + 1) * BANK)
-            nc.sync.dma_start(out=w_raw[:, :, cols], in_=w_view[:, :, cols])
+            w_raw[c] = w_pool.tile([P, H, BANK], BF16, name="w_chunk")
+            nc.sync.dma_start(out=w_raw[c][:], in_=w_view[:, :, cols])
 
         def load_r(t):
             nc.sync.dma_start(out=r_sb[:, t, :], in_=r_view[:, t, :])
@@ -75,7 +79,6 @@ def tile_multiheadattention_pb_kernel(tc, attn_out, residual, proj_w, proj_b, ln
         load_w(2)
         load_w(3)
         load_r(0)
-        nc.sync.dma_start(out=bias_bc[:], in_=proj_b.partition_broadcast(P))
         load_x(2)
         load_x(4)
         load_x(6)
@@ -100,9 +103,10 @@ def tile_multiheadattention_pb_kernel(tc, attn_out, residual, proj_w, proj_b, ln
         x_grouped = keep.tile([P, NT, P, H], BF16, align_bytes=64)
         x_codes = keep.tile([P, NT * P], U32, align_bytes=64)
         x_scales = keep.tile([P, NT * P], U8, align_bytes=64)
-        w_grouped = keep.tile([P, D, H], BF16, align_bytes=64)
+        w_grouped = {}
         w_codes = keep.tile([P, D], U32, align_bytes=64)
         w_scales = keep.tile([P, D], U8, align_bytes=64)
+        bias_col = keep.tile([P, NF], BF16)
         gain_col = keep.tile([P, NF], F32)
         out_view = out.rearrange("(p t) n -> p t n", t=NT)
 
@@ -130,21 +134,39 @@ def tile_multiheadattention_pb_kernel(tc, attn_out, residual, proj_w, proj_b, ln
             nc.vector.quantize_mx(out=x_codes[:, toks].bitcast(FP8X4), scales=x_scales[:, toks], in_=x_grouped_pair(t0))
 
         def w_group(c, copy, first=0, last=BANK):
-            cols = slice(c * BANK + first, c * BANK + last)
-            copy(out=w_grouped[:, cols, :], in_=w_raw[:, :, cols].rearrange("q i n -> q n i"))
+            if c not in w_grouped:
+                w_grouped[c] = w_pool.tile([P, BANK, H], BF16, name="w_words", align_bytes=64)
+            copy(
+                out=w_grouped[c][:, first:last, :].rearrange("q (m n) i -> q m i n", n=4),
+                in_=w_raw[c][:, :, first:last].rearrange("q i (m n) -> q m i n", n=4),
+            )
 
         def w_quantise(c):
             cols = slice(c * BANK, (c + 1) * BANK)
             nc.vector.quantize_mx(
                 out=w_codes[:, cols].bitcast(FP8X4),
                 scales=w_scales[:, cols],
-                in_=w_grouped[:, cols, :].rearrange("q n i -> q (n i)"),
+                in_=w_grouped[c][:].rearrange("q n i -> q (n i)"),
             )
 
-        def turn_gain():
+        def turn_vectors():
             rows_ps = psum_o.tile([P, P], BF16, name="rows_ps", tag="o")
-            nc.tensor.transpose(rows_ps[:], gain_rows[:], ident_b[:])
-            nc.vector.tensor_copy(out=gain_col[:], in_=rows_ps[:, 0:NF])
+            nc.tensor.transpose(rows_ps[:], vec_rows[:], ident_b[:])
+            nc.vector.tensor_copy(out=bias_col[:], in_=rows_ps[:, 0:NF])
+            nc.vector.tensor_copy(out=gain_col[:], in_=rows_ps[:, NF : 2 * NF])
+
+        spread_of = {}
+
+        def spread_bias(half):
+            spread_of[half] = psum_z.tile([P, D // 2], BF16, name="spread", tag="z")
+            for k in range(NF // 2):
+                j = half * (NF // 2) + k
+                nc.tensor.transpose(
+                    spread_of[half][:, k * P : (k + 1) * P], bias_col[:, j : j + 1].to_broadcast([P, P]), ident_b[:]
+                )
+
+        def keep_bias(half):
+            nc.scalar.copy(out=bias_bc[:, half * (D // 2) : (half + 1) * (D // 2)], in_=spread_of[half][:])
 
         rb_of = {}
         y_of = {}
@@ -204,14 +226,24 @@ def tile_multiheadattention_pb_kernel(tc, attn_out, residual, proj_w, proj_b, ln
             nc.scalar.activation(
                 out=parts[:], in_=sums_of[i][:], func=ACT.Copy, scale=-1.0 / D, accum_out=neg_mean[:]
             )
-            if i == NT - 1:
-                return
             centred_of[i] = pairs.tile([P, D], F32, name="centred")
             for c in CHUNK_ORDER:
                 cols = slice(c * BANK, (c + 1) * BANK)
-                nc.scalar.activation(
-                    out=centred_of[i][:, cols], in_=y_of[i][:, cols], func=ACT.Identity, bias=neg_mean[:], scale=1.0
-                )
+                if c in SCALAR_CENTRES and (i < NT - 1 or c in TURNED_LAST):
+                    nc.scalar.activation(
+                        out=centred_of[i][:, cols], in_=y_of[i][:, cols], func=ACT.Identity, bias=neg_mean[:], scale=1.0
+                    )
+
+        def centre_gpsimd(i, c):
+            cols = slice(c * BANK, (c + 1) * BANK)
+            nc.gpsimd.tensor_scalar(
+                out=centred_of[i][:, cols],
+                in0=y_of[i][:, cols],
+                scalar1=1.0,
+                scalar2=neg_mean_of[i][:],
+                op0=ALU.mult,
+                op1=ALU.add,
+            )
 
         def deviation(i):
             squares = pairs.tile([P, D], BF16, name="squares")
@@ -229,6 +261,28 @@ def tile_multiheadattention_pb_kernel(tc, attn_out, residual, proj_w, proj_b, ln
         def keep_clock(bank):
             nc.tensor.matmul(out=bank, lhsT=ident_f[:], rhs=ident_f[:], start=True, stop=True)
 
+        def turn_uncentred(i, c):
+            turned_of[i, c] = psum_c.tile([P, F_PER_CHUNK, P], F32, name="turned", tag="c")
+            for jj in range(F_PER_CHUNK):
+                j = c * F_PER_CHUNK + jj
+                nc.tensor.matmul(
+                    out=turned_of[i, c][:, jj, :],
+                    lhsT=y_of[i][:, j * P : (j + 1) * P],
+                    rhs=ident_f[:],
+                    start=(jj == 0),
+                    stop=False,
+                    is_transpose=True,
+                )
+
+        def subtract_mean(i, c):
+            nc.tensor.matmul(
+                out=turned_of[i, c][:],
+                lhsT=neg_mean_of[i][:].to_broadcast([P, P]),
+                rhs=ident_f[:].unsqueeze(1).to_broadcast([P, F_PER_CHUNK, P]),
+                start=False,
+                stop=True,
+            )
+
         def turn(i, c, warm=False):
             turned_of[i, c] = psum_c.tile([P, F_PER_CHUNK, P], F32, name="turned", tag="c")
             if warm:
@@ -237,18 +291,19 @@ def tile_multiheadattention_pb_kernel(tc, attn_out, residual, proj_w, proj_b, ln
                 j = c * F_PER_CHUNK + jj
                 nc.tensor.transpose(turned_of[i, c][:, jj, :], centred_of[i][:, j * P : (j + 1) * P], ident_f[:])
 
-        def scale(i, c):
-            scaled_of[i, c] = cols_pool.tile([P, F_PER_CHUNK, P], F32, name="scaled")
-            if c in VECTOR_SCALES:
-                gains = gain_col[:, c * F_PER_CHUNK : (c + 1) * F_PER_CHUNK]
+        def scale(i, c, engine, first=0, last=F_PER_CHUNK):
+            if (i, c) not in scaled_of:
+                scaled_of[i, c] = cols_pool.tile([P, F_PER_CHUNK, P], F32, name="scaled")
+            if engine is nc.vector:
+                gains = gain_col[:, c * F_PER_CHUNK + first : c * F_PER_CHUNK + last]
                 nc.vector.tensor_tensor(
-                    out=scaled_of[i, c][:],
-                    in0=turned_of[i, c][:],
-                    in1=gains.unsqueeze(2).to_broadcast([P, F_PER_CHUNK, P]),
+                    out=scaled_of[i, c][:, first:last, :],
+                    in0=turned_of[i, c][:, first:last, :],
+                    in1=gains.unsqueeze(2).to_broadcast([P, last - first, P]),
                     op=ALU.mult,
                 )
                 return
-            for jj in range(F_PER_CHUNK):
+            for jj in range(first, last):
                 j = c * F_PER_CHUNK + jj
                 nc.scalar.activation(
                     out=scaled_of[i, c][:, jj, :], in_=turned_of[i, c][:, jj, :], func=ACT.Copy, scale=gain_col[:, j : j + 1]
@@ -263,8 +318,14 @@ def tile_multiheadattention_pb_kernel(tc, attn_out, residual, proj_w, proj_b, ln
 
         def scale_last(i):
             o_of[i] = work.tile([P, D], F32, name="o")
+            cols = slice(len(TURNED_LAST) * BANK, D)
             nc.vector.scalar_tensor_tensor(
-                out=o_of[i][:], in0=y_of[i][:], scalar=neg_mean_of[i][:], in1=gain_bc[:], op0=ALU.add, op1=ALU.mult
+                out=o_of[i][:, cols],
+                in0=y_of[i][:, cols],
+                scalar=neg_mean_of[i][:],
+                in1=gain_bc[:, cols],
+                op0=ALU.add,
+                op1=ALU.mult,
             )
 
         def finish_last(i, c):
@@ -280,7 +341,7 @@ def tile_multiheadattention_pb_kernel(tc, attn_out, residual, proj_w, proj_b, ln
             nc.sync.dma_start(out=out_view[:, i, cols], in_=o_of[i][:, cols])
 
         def finish(i, c):
-            if c == CHUNK_ORDER[0]:
+            if i not in o_of:
                 o_of[i] = work.tile([P, D], F32, name="o")
             cols = slice(c * BANK, (c + 1) * BANK)
             nc.vector.scalar_tensor_tensor(
@@ -291,14 +352,19 @@ def tile_multiheadattention_pb_kernel(tc, attn_out, residual, proj_w, proj_b, ln
                 op0=ALU.mult,
                 op1=ALU.add,
             )
-            if c == CHUNK_ORDER[-1]:
-                nc.sync.dma_start(out=out_view[:, i, :], in_=o_of[i][:])
+            if i == NT - 1:
+                nc.sync.dma_start(out=out_view[:, i, cols], in_=o_of[i][:, cols])
+            elif c in (1, 3):
+                half = slice((c - 1) * BANK, (c + 1) * BANK)
+                nc.sync.dma_start(out=out_view[:, i, half], in_=o_of[i][:, half])
 
         ctx.enter_context(tc.manual_schedule())
-        turn_gain()
         x_order(0, nc.vector.tensor_copy)
         x_order(1, nc.vector.tensor_copy)
+        turn_vectors()
         x_turn(0)
+        spread_bias(0)
+        spread_bias(1)
         w_group(0, nc.vector.tensor_copy)
         w_quantise(0)
         w_group(1, nc.scalar.copy)
@@ -309,6 +375,8 @@ def tile_multiheadattention_pb_kernel(tc, attn_out, residual, proj_w, proj_b, ln
         multiply(0, 2)
         w_group(3, nc.vector.tensor_copy, 0, 256)
         w_group(3, nc.scalar.copy, 256, BANK)
+        keep_bias(0)
+        keep_bias(1)
         w_quantise(1)
         multiply(0, 1)
         w_quantise(3)
@@ -339,13 +407,15 @@ def tile_multiheadattention_pb_kernel(tc, attn_out, residual, proj_w, proj_b, ln
                 x_quantise(4)
             if s == 2:
                 x_quantise(6)
+            if s < NT:
+                turn_uncentred(s - 1, 2)
+                subtract_mean(s - 1, 2)
             if s >= 2:
                 invert(s - 2)
                 finish(s - 2, 2)
-                turn_back(s - 2, 0, warm=True)
+                turn_back(s - 2, 0)
             if s < NT:
                 add(s, 0)
-                turn(s - 1, 2)
             if s >= 2:
                 finish(s - 2, 3)
                 turn_back(s - 2, 1)
@@ -358,25 +428,31 @@ def tile_multiheadattention_pb_kernel(tc, attn_out, residual, proj_w, proj_b, ln
                 multiply(s + 1, 0)
                 multiply(s + 1, 1)
             if s < NT:
-                scale(s - 1, 2)
+                scale(s - 1, 2, nc.vector)
             if s >= 2:
                 finish(s - 2, 0)
             if s < NT:
                 add(s, 2)
-                turn(s - 1, 0, warm=True)
-                scale(s - 1, 3)
-                turn(s - 1, 1)
+            turn(s - 1, 0, warm=True)
+            if s < NT:
+                turn_back(s - 1, 2, warm=True)
+                scale(s - 1, 3, nc.vector, 0, 2)
+                scale(s - 1, 3, nc.scalar, 2)
+            turn(s - 1, 1)
             if s >= 2:
                 finish(s - 2, 1)
             if s < NT:
                 add(s, 3)
-                turn_back(s - 1, 2, warm=True)
                 turn_back(s - 1, 3)
-                scale(s - 1, 0)
-                scale(s - 1, 1)
+            scale(s - 1, 0, nc.scalar)
+            scale(s - 1, 1, nc.scalar)
             if s + 1 < NT:
                 multiply(s + 1, 2)
                 multiply(s + 1, 3)
         invert(NT - 1)
-        for c in range(NC):
+        for c in TURNED_LAST:
+            turn_back(NT - 1, c)
+        for c in range(len(TURNED_LAST), NC):
             finish_last(NT - 1, c)
+        for c in TURNED_LAST:
+            finish(NT - 1, c)

@@ -23,7 +23,9 @@ NC = D // BANK
 F_PER_CHUNK = BANK // P
 LN_EPS = 1e-5
 CHUNK_ORDER = (2, 3, 0, 1)
-SCALAR_CENTRES = (3, 0, 1)
+HALF = 2
+HALVES = (2, 3, 0)
+SCALAR_CENTRES = (2, 3, 0, 1)
 TURNED_LAST = (0,)
 REPEATS = (1, 1)
 
@@ -228,7 +230,7 @@ def tile_multiheadattention_pb_kernel(tc, attn_out, residual, proj_w, proj_b, ln
             )
             centred_of[i] = pairs.tile([P, D], F32, name="centred")
             for c in CHUNK_ORDER:
-                cols = slice(c * BANK, (c + 1) * BANK)
+                cols = slice(c * BANK + (HALF * P if c in HALVES and i < NT - 1 else 0), (c + 1) * BANK)
                 if c in SCALAR_CENTRES and (i < NT - 1 or c in TURNED_LAST):
                     nc.scalar.activation(
                         out=centred_of[i][:, cols], in_=y_of[i][:, cols], func=ACT.Identity, bias=neg_mean[:], scale=1.0
@@ -261,9 +263,9 @@ def tile_multiheadattention_pb_kernel(tc, attn_out, residual, proj_w, proj_b, ln
         def keep_clock(bank):
             nc.tensor.matmul(out=bank, lhsT=ident_f[:], rhs=ident_f[:], start=True, stop=True)
 
-        def turn_uncentred(i, c):
+        def turn_half(i, c):
             turned_of[i, c] = psum_c.tile([P, F_PER_CHUNK, P], F32, name="turned", tag="c")
-            for jj in range(F_PER_CHUNK):
+            for jj in range(HALF):
                 j = c * F_PER_CHUNK + jj
                 nc.tensor.matmul(
                     out=turned_of[i, c][:, jj, :],
@@ -273,15 +275,16 @@ def tile_multiheadattention_pb_kernel(tc, attn_out, residual, proj_w, proj_b, ln
                     stop=False,
                     is_transpose=True,
                 )
-
-        def subtract_mean(i, c):
             nc.tensor.matmul(
-                out=turned_of[i, c][:],
+                out=turned_of[i, c][:, 0:HALF, :],
                 lhsT=neg_mean_of[i][:].to_broadcast([P, P]),
-                rhs=ident_f[:].unsqueeze(1).to_broadcast([P, F_PER_CHUNK, P]),
+                rhs=ident_f[:].unsqueeze(1).to_broadcast([P, HALF, P]),
                 start=False,
                 stop=True,
             )
+            for jj in range(HALF, F_PER_CHUNK):
+                j = c * F_PER_CHUNK + jj
+                nc.tensor.transpose(turned_of[i, c][:, jj, :], centred_of[i][:, j * P : (j + 1) * P], ident_f[:])
 
         def turn(i, c, warm=False):
             turned_of[i, c] = psum_c.tile([P, F_PER_CHUNK, P], F32, name="turned", tag="c")
@@ -408,8 +411,7 @@ def tile_multiheadattention_pb_kernel(tc, attn_out, residual, proj_w, proj_b, ln
             if s == 2:
                 x_quantise(6)
             if s < NT:
-                turn_uncentred(s - 1, 2)
-                subtract_mean(s - 1, 2)
+                turn_half(s - 1, 2)
             if s >= 2:
                 invert(s - 2)
                 finish(s - 2, 2)
@@ -421,7 +423,7 @@ def tile_multiheadattention_pb_kernel(tc, attn_out, residual, proj_w, proj_b, ln
                 turn_back(s - 2, 1)
             if s < NT:
                 add(s, 1)
-                turn(s - 1, 3)
+                turn_half(s - 1, 3)
             else:
                 scale_last(s - 1)
             if s + 1 < NT:
@@ -433,19 +435,24 @@ def tile_multiheadattention_pb_kernel(tc, attn_out, residual, proj_w, proj_b, ln
                 finish(s - 2, 0)
             if s < NT:
                 add(s, 2)
-            turn(s - 1, 0, warm=True)
             if s < NT:
-                turn_back(s - 1, 2, warm=True)
+                turn_half(s - 1, 0)
+            else:
+                turn(s - 1, 0)
+            if s < NT:
+                turn_back(s - 1, 2)
                 scale(s - 1, 3, nc.vector, 0, 2)
                 scale(s - 1, 3, nc.scalar, 2)
-            turn(s - 1, 1)
+            if s < NT:
+                turn(s - 1, 1)
             if s >= 2:
                 finish(s - 2, 1)
             if s < NT:
                 add(s, 3)
                 turn_back(s - 1, 3)
             scale(s - 1, 0, nc.scalar)
-            scale(s - 1, 1, nc.scalar)
+            if s < NT:
+                scale(s - 1, 1, nc.scalar)
             if s + 1 < NT:
                 multiply(s + 1, 2)
                 multiply(s + 1, 3)

@@ -25,7 +25,7 @@ LN_EPS = 1e-5
 CHUNK_ORDER = (2, 3, 0, 1)
 HALF = 2
 HALVES = (2, 3, 0)
-SCALAR_CENTRES = (2, 3, 0, 1)
+SCALAR_CENTRES = (2, 3, 0)
 TURNED_LAST = (0,)
 REPEATS = (1, 1)
 
@@ -175,6 +175,7 @@ def tile_multiheadattention_pb_kernel(tc, attn_out, residual, proj_w, proj_b, ln
         sums_of = {}
         z_of = {}
         neg_mean_of = {}
+        sq_sum_of = {}
         std_of = {}
         centred_of = {}
         turned_of = {}
@@ -222,22 +223,25 @@ def tile_multiheadattention_pb_kernel(tc, attn_out, residual, proj_w, proj_b, ln
                 accum_out=sums_of[i][:, c : c + 1],
             )
 
-        def centre(i):
+        def mean(i):
             neg_mean = neg_mean_of[i] = small.tile([P, 1], F32, name="neg_mean")
             parts = small.tile([P, NC], F32, name="parts")
             nc.scalar.activation(
                 out=parts[:], in_=sums_of[i][:], func=ACT.Copy, scale=-1.0 / D, accum_out=neg_mean[:]
             )
+
+        def centre(i):
+            neg_mean = neg_mean_of[i]
             centred_of[i] = pairs.tile([P, D], F32, name="centred")
             for c in CHUNK_ORDER:
-                cols = slice(c * BANK + (HALF * P if c in HALVES and i < NT - 1 else 0), (c + 1) * BANK)
+                cols = slice(c * BANK + (HALF * P if c in HALVES and i < NT - 1 else 0), (c + 1) * BANK - (4 * P if c == 1 else 0))
                 if c in SCALAR_CENTRES and (i < NT - 1 or c in TURNED_LAST):
                     nc.scalar.activation(
                         out=centred_of[i][:, cols], in_=y_of[i][:, cols], func=ACT.Identity, bias=neg_mean[:], scale=1.0
                     )
 
         def centre_gpsimd(i, c):
-            cols = slice(c * BANK, (c + 1) * BANK)
+            cols = slice(c * BANK + 0 * P, (c + 1) * BANK)
             nc.gpsimd.tensor_scalar(
                 out=centred_of[i][:, cols],
                 in0=y_of[i][:, cols],
@@ -253,8 +257,11 @@ def tile_multiheadattention_pb_kernel(tc, attn_out, residual, proj_w, proj_b, ln
             nc.scalar.activation(
                 out=squares[:], in_=y_of[i][:], func=ACT.Square, bias=neg_mean_of[i][:], scale=1.0, accum_out=sq_sum[:]
             )
+            sq_sum_of[i] = sq_sum
+
+        def root(i):
             std_of[i] = small.tile([P, 1], F32, name="std")
-            nc.scalar.activation(out=std_of[i][:], in_=sq_sum[:], func=ACT.Sqrt, bias=eps[:], scale=1.0 / D)
+            nc.scalar.activation(out=std_of[i][:], in_=sq_sum_of[i][:], func=ACT.Sqrt, bias=eps[:], scale=1.0 / D)
 
         def invert(i):
             rstd_of[i] = small.tile([P, 1], F32, name="rstd")
@@ -401,10 +408,15 @@ def tile_multiheadattention_pb_kernel(tc, attn_out, residual, proj_w, proj_b, ln
         multiply(1, 3)
         residual_and_bias(1, nc.gpsimd)
 
+        mean(0)
         for s in range(1, NT + 1):
-            if s + 1 < NT:
-                residual_and_bias(s + 1, nc.gpsimd)
             centre(s - 1)
+            if s + 1 < NT:
+                residual_and_bias(s + 1, nc.gpsimd, range(0))
+            if s < NT:
+                centre_gpsimd(s - 1, 1)
+            if s + 1 < NT:
+                residual_and_bias(s + 1, nc.gpsimd, range(0, NC))
             deviation(s - 1)
             if s == 1:
                 x_quantise(4)
@@ -412,12 +424,11 @@ def tile_multiheadattention_pb_kernel(tc, attn_out, residual, proj_w, proj_b, ln
                 x_quantise(6)
             if s < NT:
                 turn_half(s - 1, 2)
-            if s >= 2:
-                invert(s - 2)
-                finish(s - 2, 2)
-                turn_back(s - 2, 0)
             if s < NT:
                 add(s, 0)
+            if s >= 2:
+                finish(s - 2, 2)
+                turn_back(s - 2, 0)
             if s >= 2:
                 finish(s - 2, 3)
                 turn_back(s - 2, 1)
@@ -441,18 +452,24 @@ def tile_multiheadattention_pb_kernel(tc, attn_out, residual, proj_w, proj_b, ln
                 turn(s - 1, 0)
             if s < NT:
                 turn_back(s - 1, 2)
-                scale(s - 1, 3, nc.vector, 0, 2)
-                scale(s - 1, 3, nc.scalar, 2)
+                scale(s - 1, 3, nc.vector, 0, 1)
+                scale(s - 1, 3, nc.scalar, 1, 3)
+            root(s - 1)
+            if s < NT:
+                scale(s - 1, 3, nc.scalar, 3)
             if s < NT:
                 turn(s - 1, 1)
             if s >= 2:
                 finish(s - 2, 1)
             if s < NT:
                 add(s, 3)
+                invert(s - 1)
                 turn_back(s - 1, 3)
             scale(s - 1, 0, nc.scalar)
             if s < NT:
-                scale(s - 1, 1, nc.scalar)
+                scale(s - 1, 1, nc.scalar, 0, 3)
+                mean(s)
+                scale(s - 1, 1, nc.scalar, 3)
             if s + 1 < NT:
                 multiply(s + 1, 2)
                 multiply(s + 1, 3)

@@ -25,7 +25,7 @@ LN_EPS = 1e-5
 CHUNK_ORDER = (2, 3, 0, 1)
 HALF = 2
 HALVES = (2, 3, 0)
-SCALAR_CENTRES = (2, 3, 0)
+SCALAR_CENTRES = (2, 3, 0, 1)
 TURNED_LAST = (0,)
 REPEATS = (1, 1)
 
@@ -234,14 +234,14 @@ def tile_multiheadattention_pb_kernel(tc, attn_out, residual, proj_w, proj_b, ln
             neg_mean = neg_mean_of[i]
             centred_of[i] = pairs.tile([P, D], F32, name="centred")
             for c in CHUNK_ORDER:
-                cols = slice(c * BANK + (HALF * P if c in HALVES and i < NT - 1 else 0), (c + 1) * BANK - (4 * P if c == 1 else 0))
+                cols = slice(c * BANK + (HALF * P if c in HALVES and i < NT - 1 else 0), (c + 1) * BANK - (2 * P if c == 1 else 0))
                 if c in SCALAR_CENTRES and (i < NT - 1 or c in TURNED_LAST):
                     nc.scalar.activation(
                         out=centred_of[i][:, cols], in_=y_of[i][:, cols], func=ACT.Identity, bias=neg_mean[:], scale=1.0
                     )
 
         def centre_gpsimd(i, c):
-            cols = slice(c * BANK + 0 * P, (c + 1) * BANK)
+            cols = slice(c * BANK + 2 * P, (c + 1) * BANK)
             nc.gpsimd.tensor_scalar(
                 out=centred_of[i][:, cols],
                 in0=y_of[i][:, cols],
@@ -452,8 +452,8 @@ def tile_multiheadattention_pb_kernel(tc, attn_out, residual, proj_w, proj_b, ln
                 turn(s - 1, 0)
             if s < NT:
                 turn_back(s - 1, 2)
-                scale(s - 1, 3, nc.vector, 0, 1)
-                scale(s - 1, 3, nc.scalar, 1, 3)
+                scale(s - 1, 3, nc.vector, 0, 2)
+                scale(s - 1, 3, nc.scalar, 2, 3)
             root(s - 1)
             if s < NT:
                 scale(s - 1, 3, nc.scalar, 3)

@@ -189,9 +189,11 @@ def tile_multiheadattention_pb_kernel(tc, attn_out, residual, proj_w, proj_b, ln
                 rb_of[i] = work.tile([P, D], F32, name="rb")
             for c in chunks:
                 cols = slice(c * BANK, (c + 1) * BANK)
-                engine.tensor_tensor(
-                    out=rb_of[i][:, cols], in0=r_sb[:, i, cols], in1=bias_bc[:, cols], op=ALU.add
-                )
+                if engine is nc.vector:
+                    bias = spread_of[c // 2][:, c % 2 * BANK : (c % 2 + 1) * BANK]
+                else:
+                    bias = bias_bc[:, cols]
+                engine.tensor_tensor(out=rb_of[i][:, cols], in0=r_sb[:, i, cols], in1=bias, op=ALU.add)
 
         def multiply(i, c):
             toks = slice(i * P, (i + 1) * P)

@@ -22,10 +22,11 @@ BANK = 512
 NC = D // BANK
 F_PER_CHUNK = BANK // P
 LN_EPS = 1e-5
-CHUNK_ORDER = (2, 3, 0, 1)
+CHUNK_ORDER = (2, 0, 1)
+DIRECT = 3
 HALF = 2
-HALVES = (2, 3, 0)
-SCALAR_CENTRES = (2, 3, 0, 1)
+HALVES = (2, 0, 1)
+SCALAR_CENTRES = (2, 0)
 TURNED_LAST = (0,)
 REPEATS = (1, 1)
 
@@ -39,10 +40,12 @@ def tile_multiheadattention_pb_kernel(tc, attn_out, residual, proj_w, proj_b, ln
         x_pool = ctx.enter_context(tc.tile_pool(name="x_pool", bufs=NT // 2))
         w_pool = ctx.enter_context(tc.tile_pool(name="w_pool", bufs=NC))
         work = ctx.enter_context(tc.tile_pool(name="work", bufs=3))
+        rb_pool = ctx.enter_context(tc.tile_pool(name="rb_pool", bufs=5))
         cols_pool = ctx.enter_context(tc.tile_pool(name="cols_pool", bufs=8))
         pairs = ctx.enter_context(tc.tile_pool(name="pairs", bufs=2))
         small = ctx.enter_context(tc.tile_pool(name="small", bufs=4))
-        psum_z = ctx.enter_context(tc.psum_pool(name="psum_z", bufs=4))
+        psum_k = ctx.enter_context(tc.psum_pool(name="psum_k", bufs=1))
+        psum_z = ctx.enter_context(tc.psum_pool(name="psum_z", bufs=3))
         psum_c = ctx.enter_context(tc.psum_pool(name="psum_c", bufs=2))
         psum_o = ctx.enter_context(tc.psum_pool(name="psum_o", bufs=2))
 
@@ -50,6 +53,7 @@ def tile_multiheadattention_pb_kernel(tc, attn_out, residual, proj_w, proj_b, ln
         nc.vector.memset(vec_rows[:], 0.0)
         nc.sync.dma_start(out=vec_rows[0:NF, :], in_=proj_b.rearrange("(j q) -> j q", q=P))
         nc.sync.dma_start(out=vec_rows[NF : 2 * NF, :], in_=ln_g.rearrange("(j q) -> j q", q=P))
+        nc.sync.dma_start(out=vec_rows[2 * NF : 3 * NF, :], in_=ln_b.rearrange("(j q) -> j q", q=P))
         bias_bc = keep.tile([P, D], BF16)
         x_raw = {}
         x_view = attn_out.rearrange("h (p t) j -> p h t j", t=NT)
@@ -82,9 +86,9 @@ def tile_multiheadattention_pb_kernel(tc, attn_out, residual, proj_w, proj_b, ln
         load_w(3)
         load_r(0)
         load_x(2)
+        load_r(1)
         load_x(4)
         load_x(6)
-        load_r(1)
         load_r(2)
         nc.sync.dma_start(out=shift_bc[:], in_=ln_b.partition_broadcast(P))
         for t in range(3, NT):
@@ -109,6 +113,7 @@ def tile_multiheadattention_pb_kernel(tc, attn_out, residual, proj_w, proj_b, ln
         w_codes = keep.tile([P, D], U32, align_bytes=64)
         w_scales = keep.tile([P, D], U8, align_bytes=64)
         bias_col = keep.tile([P, NF], BF16)
+        vec_col = keep.tile([P, 2 * NF], BF16)
         gain_col = keep.tile([P, NF], F32)
         out_view = out.rearrange("(p t) n -> p t n", t=NT)
 
@@ -156,16 +161,27 @@ def tile_multiheadattention_pb_kernel(tc, attn_out, residual, proj_w, proj_b, ln
             nc.tensor.transpose(rows_ps[:], vec_rows[:], ident_b[:])
             nc.vector.tensor_copy(out=bias_col[:], in_=rows_ps[:, 0:NF])
             nc.vector.tensor_copy(out=gain_col[:], in_=rows_ps[:, NF : 2 * NF])
+            nc.vector.tensor_copy(out=vec_col[:], in_=rows_ps[:, NF : 3 * NF])
 
         spread_of = {}
 
         def spread_bias(half):
-            spread_of[half] = psum_z.tile([P, D // 2], BF16, name="spread", tag="z")
+            spread_of[half] = psum_o.tile([P, D // 2], BF16, name="spread", tag="o")
             for k in range(NF // 2):
                 j = half * (NF // 2) + k
                 nc.tensor.transpose(
                     spread_of[half][:, k * P : (k + 1) * P], bias_col[:, j : j + 1].to_broadcast([P, P]), ident_b[:]
                 )
+
+        direct = psum_k.tile([P, 2, BANK], BF16, name="direct")
+
+        def spread_direct():
+            for v in range(2):
+                for jj in range(F_PER_CHUNK):
+                    j = v * NF + DIRECT * F_PER_CHUNK + jj
+                    nc.tensor.transpose(
+                        direct[:, v, jj * P : (jj + 1) * P], vec_col[:, j : j + 1].to_broadcast([P, P]), ident_b[:]
+                    )
 
         def keep_bias(half):
             nc.scalar.copy(out=bias_bc[:, half * (D // 2) : (half + 1) * (D // 2)], in_=spread_of[half][:])
@@ -186,7 +202,7 @@ def tile_multiheadattention_pb_kernel(tc, attn_out, residual, proj_w, proj_b, ln
 
         def residual_and_bias(i, engine, chunks=range(NC)):
             if i not in rb_of:
-                rb_of[i] = work.tile([P, D], F32, name="rb")
+                rb_of[i] = rb_pool.tile([P, D], F32, name="rb")
             for c in chunks:
                 cols = slice(c * BANK, (c + 1) * BANK)
                 if engine is nc.vector:
@@ -340,6 +356,33 @@ def tile_multiheadattention_pb_kernel(tc, attn_out, residual, proj_w, proj_b, ln
                 op1=ALU.mult,
             )
 
+        def gain_direct(i):
+            o_of[i] = work.tile([P, D], F32, name="o")
+            cols = slice(DIRECT * BANK, (DIRECT + 1) * BANK)
+            nc.vector.scalar_tensor_tensor(
+                out=o_of[i][:, cols],
+                in0=y_of[i][:, cols],
+                scalar=neg_mean_of[i][:],
+                in1=direct[:, 0, :],
+                op0=ALU.add,
+                op1=ALU.mult,
+            )
+
+        def finish_direct(i):
+            cols = slice(DIRECT * BANK, (DIRECT + 1) * BANK)
+            nc.vector.scalar_tensor_tensor(
+                out=o_of[i][:, cols],
+                in0=o_of[i][:, cols],
+                scalar=rstd_of[i][:],
+                in1=direct[:, 1, :],
+                op0=ALU.mult,
+                op1=ALU.add,
+            )
+
+        def store(i, first, last):
+            cols = slice(first * BANK, last * BANK)
+            nc.sync.dma_start(out=out_view[:, i, cols], in_=o_of[i][:, cols])
+
         def finish_last(i, c):
             cols = slice(c * BANK, (c + 1) * BANK)
             nc.vector.scalar_tensor_tensor(
@@ -365,10 +408,7 @@ def tile_multiheadattention_pb_kernel(tc, attn_out, residual, proj_w, proj_b, ln
                 op1=ALU.add,
             )
             if i == NT - 1:
-                nc.sync.dma_start(out=out_view[:, i, cols], in_=o_of[i][:, cols])
-            elif c in (1, 3):
-                half = slice((c - 1) * BANK, (c + 1) * BANK)
-                nc.sync.dma_start(out=out_view[:, i, half], in_=o_of[i][:, half])
+                store(i, c, c + 1)
 
         ctx.enter_context(tc.manual_schedule())
         x_order(0, nc.vector.tensor_copy)
@@ -377,6 +417,7 @@ def tile_multiheadattention_pb_kernel(tc, attn_out, residual, proj_w, proj_b, ln
         x_turn(0)
         spread_bias(0)
         spread_bias(1)
+        spread_direct()
         w_group(0, nc.vector.tensor_copy)
         w_quantise(0)
         w_group(1, nc.scalar.copy)
@@ -392,7 +433,6 @@ def tile_multiheadattention_pb_kernel(tc, attn_out, residual, proj_w, proj_b, ln
         w_quantise(1)
         multiply(0, 1)
         w_quantise(3)
-        multiply(0, 3)
         for t in range(2, NT):
             x_order(t, nc.scalar.copy)
         x_turn(2)
@@ -400,6 +440,7 @@ def tile_multiheadattention_pb_kernel(tc, attn_out, residual, proj_w, proj_b, ln
         x_turn(6)
         residual_and_bias(0, nc.vector)
         add(0, 0)
+        multiply(0, 3)
         add(0, 2)
         add(0, 1)
         add(0, 3)
@@ -407,43 +448,38 @@ def tile_multiheadattention_pb_kernel(tc, attn_out, residual, proj_w, proj_b, ln
         multiply(1, 0)
         multiply(1, 1)
         multiply(1, 2)
-        multiply(1, 3)
         residual_and_bias(1, nc.gpsimd)
 
         mean(0)
         for s in range(1, NT + 1):
             centre(s - 1)
-            if s + 1 < NT:
-                residual_and_bias(s + 1, nc.gpsimd, range(0))
             if s < NT:
                 centre_gpsimd(s - 1, 1)
             if s + 1 < NT:
-                residual_and_bias(s + 1, nc.gpsimd, range(0, NC))
+                residual_and_bias(s + 1, nc.gpsimd)
+            if s < NT:
+                turn_half(s - 1, 2)
             deviation(s - 1)
             if s == 1:
                 x_quantise(4)
             if s == 2:
                 x_quantise(6)
             if s < NT:
-                turn_half(s - 1, 2)
-            if s < NT:
                 add(s, 0)
             if s >= 2:
+                finish_direct(s - 2)
                 finish(s - 2, 2)
+                store(s - 2, 2, 4)
                 turn_back(s - 2, 0)
-            if s >= 2:
-                finish(s - 2, 3)
                 turn_back(s - 2, 1)
             if s < NT:
                 add(s, 1)
-                turn_half(s - 1, 3)
+                gain_direct(s - 1)
+                multiply(s, 3)
             else:
                 scale_last(s - 1)
             if s + 1 < NT:
                 multiply(s + 1, 0)
-                multiply(s + 1, 1)
-            if s < NT:
-                scale(s - 1, 2, nc.vector)
             if s >= 2:
                 finish(s - 2, 0)
             if s < NT:
@@ -453,28 +489,27 @@ def tile_multiheadattention_pb_kernel(tc, attn_out, residual, proj_w, proj_b, ln
             else:
                 turn(s - 1, 0)
             if s < NT:
-                turn_back(s - 1, 2)
-                scale(s - 1, 3, nc.vector, 0, 2)
-                scale(s - 1, 3, nc.scalar, 2, 3)
+                scale(s - 1, 2, nc.scalar, 0, 2)
             root(s - 1)
             if s < NT:
-                scale(s - 1, 3, nc.scalar, 3)
+                scale(s - 1, 2, nc.scalar, 2)
             if s < NT:
-                turn(s - 1, 1)
+                turn_half(s - 1, 1)
             if s >= 2:
                 finish(s - 2, 1)
+                store(s - 2, 0, 2)
             if s < NT:
                 add(s, 3)
                 invert(s - 1)
-                turn_back(s - 1, 3)
+                turn_back(s - 1, 2)
             scale(s - 1, 0, nc.scalar)
             if s < NT:
                 scale(s - 1, 1, nc.scalar, 0, 3)
                 mean(s)
                 scale(s - 1, 1, nc.scalar, 3)
             if s + 1 < NT:
+                multiply(s + 1, 1)
                 multiply(s + 1, 2)
-                multiply(s + 1, 3)
         invert(NT - 1)
         for c in TURNED_LAST:
             turn_back(NT - 1, c)

@@ -25,8 +25,7 @@ LN_EPS = 1e-5
 CHUNK_ORDER = (2, 0, 1)
 DIRECT = 3
 HALF = 2
-HALVES = (2, 0, 1)
-SCALAR_CENTRES = (2, 0)
+CENTRING = {2: ("product", "scalar"), 0: ("product", "scalar"), 1: ("transpose", "transpose")}
 TURNED_LAST = (0,)
 REPEATS = (1, 1)
 
@@ -252,22 +251,12 @@ def tile_multiheadattention_pb_kernel(tc, attn_out, residual, proj_w, proj_b, ln
             neg_mean = neg_mean_of[i]
             centred_of[i] = pairs.tile([P, D], F32, name="centred")
             for c in CHUNK_ORDER:
-                cols = slice(c * BANK + (HALF * P if c in HALVES and i < NT - 1 else 0), (c + 1) * BANK - (2 * P if c == 1 else 0))
-                if c in SCALAR_CENTRES and (i < NT - 1 or c in TURNED_LAST):
-                    nc.scalar.activation(
-                        out=centred_of[i][:, cols], in_=y_of[i][:, cols], func=ACT.Identity, bias=neg_mean[:], scale=1.0
-                    )
-
-        def centre_gpsimd(i, c):
-            cols = slice(c * BANK + 2 * P, (c + 1) * BANK)
-            nc.gpsimd.tensor_scalar(
-                out=centred_of[i][:, cols],
-                in0=y_of[i][:, cols],
-                scalar1=1.0,
-                scalar2=neg_mean_of[i][:],
-                op0=ALU.mult,
-                op1=ALU.add,
-            )
+                for h in range(2):
+                    if i < NT - 1 and CENTRING[c][h] == "scalar" or i == NT - 1 and c in TURNED_LAST:
+                        cols = slice(c * BANK + h * HALF * P, c * BANK + (h + 1) * HALF * P)
+                        nc.scalar.activation(
+                            out=centred_of[i][:, cols], in_=y_of[i][:, cols], func=ACT.Identity, bias=neg_mean[:], scale=1.0
+                        )
 
         def deviation(i):
             squares = pairs.tile([P, D], BF16, name="squares")
@@ -290,26 +279,39 @@ def tile_multiheadattention_pb_kernel(tc, attn_out, residual, proj_w, proj_b, ln
 
         def turn_half(i, c):
             turned_of[i, c] = psum_c.tile([P, F_PER_CHUNK, P], F32, name="turned", tag="c")
-            for jj in range(HALF):
-                j = c * F_PER_CHUNK + jj
-                nc.tensor.matmul(
-                    out=turned_of[i, c][:, jj, :],
-                    lhsT=y_of[i][:, j * P : (j + 1) * P],
-                    rhs=ident_f[:],
-                    start=(jj == 0),
-                    stop=False,
-                    is_transpose=True,
-                )
-            nc.tensor.matmul(
-                out=turned_of[i, c][:, 0:HALF, :],
-                lhsT=neg_mean_of[i][:].to_broadcast([P, P]),
-                rhs=ident_f[:].unsqueeze(1).to_broadcast([P, HALF, P]),
-                start=False,
-                stop=True,
-            )
-            for jj in range(HALF, F_PER_CHUNK):
-                j = c * F_PER_CHUNK + jj
-                nc.tensor.transpose(turned_of[i, c][:, jj, :], centred_of[i][:, j * P : (j + 1) * P], ident_f[:])
+            for h in range(2):
+                way = CENTRING[c][h]
+                tiles = range(h * HALF, (h + 1) * HALF)
+                source = centred_of[i] if way == "scalar" else y_of[i]
+                for jj in tiles:
+                    j = c * F_PER_CHUNK + jj
+                    nc.tensor.matmul(
+                        out=turned_of[i, c][:, jj, :],
+                        lhsT=source[:, j * P : (j + 1) * P],
+                        rhs=ident_f[:],
+                        start=(jj == tiles[0]),
+                        stop=(way == "scalar" and jj == tiles[-1]),
+                        is_transpose=True,
+                    )
+                spread_mean = neg_mean_of[i][:].to_broadcast([P, P])
+                if way == "product":
+                    nc.tensor.matmul(
+                        out=turned_of[i, c][:, h * HALF : (h + 1) * HALF, :],
+                        lhsT=spread_mean,
+                        rhs=ident_f[:].unsqueeze(1).to_broadcast([P, HALF, P]),
+                        start=False,
+                        stop=True,
+                    )
+                if way == "transpose":
+                    for jj in tiles:
+                        nc.tensor.matmul(
+                            out=turned_of[i, c][:, jj, :],
+                            lhsT=spread_mean,
+                            rhs=ident_f[:],
+                            start=False,
+                            stop=(jj == tiles[-1]),
+                            is_transpose=True,
+                        )
 
         def turn(i, c, warm=False):
             turned_of[i, c] = psum_c.tile([P, F_PER_CHUNK, P], F32, name="turned", tag="c")
@@ -439,6 +441,7 @@ def tile_multiheadattention_pb_kernel(tc, attn_out, residual, proj_w, proj_b, ln
         x_turn(4)
         x_turn(6)
         residual_and_bias(0, nc.vector)
+        residual_and_bias(1, nc.vector, range(4, NC))
         add(0, 0)
         multiply(0, 3)
         add(0, 2)
@@ -448,13 +451,11 @@ def tile_multiheadattention_pb_kernel(tc, attn_out, residual, proj_w, proj_b, ln
         multiply(1, 0)
         multiply(1, 1)
         multiply(1, 2)
-        residual_and_bias(1, nc.gpsimd)
+        residual_and_bias(1, nc.gpsimd, range(4))
 
         mean(0)
         for s in range(1, NT + 1):
             centre(s - 1)
-            if s < NT:
-                centre_gpsimd(s - 1, 1)
             if s + 1 < NT:
                 residual_and_bias(s + 1, nc.gpsimd)
             if s < NT:

@@ -25,8 +25,9 @@ LN_EPS = 1e-5
 CHUNK_ORDER = (2, 0, 1)
 DIRECT = 3
 HALF = 2
-CENTRING = {2: ("product", "scalar"), 0: ("product", "scalar"), 1: ("transpose", "transpose")}
-TURNED_LAST = (0,)
+CENTRING = {2: ("product", "scalar"), 0: ("product", "transpose"), 1: ("transpose", "transpose")}
+TURNED_LAST = (0, 1)
+CENTRING_LAST = ("transpose", "transpose")
 REPEATS = (1, 1)
 
 FLOPS = 2 * LQ * H * DV * D
@@ -252,7 +253,7 @@ def tile_multiheadattention_pb_kernel(tc, attn_out, residual, proj_w, proj_b, ln
             centred_of[i] = pairs.tile([P, D], F32, name="centred")
             for c in CHUNK_ORDER:
                 for h in range(2):
-                    if i < NT - 1 and CENTRING[c][h] == "scalar" or i == NT - 1 and c in TURNED_LAST:
+                    if i < NT - 1 and CENTRING[c][h] == "scalar":
                         cols = slice(c * BANK + h * HALF * P, c * BANK + (h + 1) * HALF * P)
                         nc.scalar.activation(
                             out=centred_of[i][:, cols], in_=y_of[i][:, cols], func=ACT.Identity, bias=neg_mean[:], scale=1.0
@@ -280,7 +281,7 @@ def tile_multiheadattention_pb_kernel(tc, attn_out, residual, proj_w, proj_b, ln
         def turn_half(i, c):
             turned_of[i, c] = psum_c.tile([P, F_PER_CHUNK, P], F32, name="turned", tag="c")
             for h in range(2):
-                way = CENTRING[c][h]
+                way = CENTRING[c][h] if i < NT - 1 else CENTRING_LAST[h]
                 tiles = range(h * HALF, (h + 1) * HALF)
                 source = centred_of[i] if way == "scalar" else y_of[i]
                 for jj in tiles:
@@ -312,14 +313,6 @@ def tile_multiheadattention_pb_kernel(tc, attn_out, residual, proj_w, proj_b, ln
                             stop=(jj == tiles[-1]),
                             is_transpose=True,
                         )
-
-        def turn(i, c, warm=False):
-            turned_of[i, c] = psum_c.tile([P, F_PER_CHUNK, P], F32, name="turned", tag="c")
-            if warm:
-                keep_clock(turned_of[i, c][:, 0, :])
-            for jj in range(F_PER_CHUNK):
-                j = c * F_PER_CHUNK + jj
-                nc.tensor.transpose(turned_of[i, c][:, jj, :], centred_of[i][:, j * P : (j + 1) * P], ident_f[:])
 
         def scale(i, c, engine, first=0, last=F_PER_CHUNK):
             if (i, c) not in scaled_of:
@@ -441,7 +434,6 @@ def tile_multiheadattention_pb_kernel(tc, attn_out, residual, proj_w, proj_b, ln
         x_turn(4)
         x_turn(6)
         residual_and_bias(0, nc.vector)
-        residual_and_bias(1, nc.vector, range(4, NC))
         add(0, 0)
         multiply(0, 3)
         add(0, 2)
@@ -451,7 +443,7 @@ def tile_multiheadattention_pb_kernel(tc, attn_out, residual, proj_w, proj_b, ln
         multiply(1, 0)
         multiply(1, 1)
         multiply(1, 2)
-        residual_and_bias(1, nc.gpsimd, range(4))
+        residual_and_bias(1, nc.gpsimd, range(NC))
 
         mean(0)
         for s in range(1, NT + 1):
@@ -472,7 +464,12 @@ def tile_multiheadattention_pb_kernel(tc, attn_out, residual, proj_w, proj_b, ln
                 finish(s - 2, 2)
                 store(s - 2, 2, 4)
                 turn_back(s - 2, 0)
+                if s == NT:
+                    turn_half(NT - 1, 0)
                 turn_back(s - 2, 1)
+                if s == NT:
+                    for c in TURNED_LAST[1:]:
+                        turn_half(NT - 1, c)
             if s < NT:
                 add(s, 1)
                 gain_direct(s - 1)
@@ -487,8 +484,6 @@ def tile_multiheadattention_pb_kernel(tc, attn_out, residual, proj_w, proj_b, ln
                 add(s, 2)
             if s < NT:
                 turn_half(s - 1, 0)
-            else:
-                turn(s - 1, 0)
             if s < NT:
                 scale(s - 1, 2, nc.scalar, 0, 2)
             root(s - 1)
@@ -503,8 +498,11 @@ def tile_multiheadattention_pb_kernel(tc, attn_out, residual, proj_w, proj_b, ln
                 add(s, 3)
                 invert(s - 1)
                 turn_back(s - 1, 2)
-            scale(s - 1, 0, nc.scalar)
+            if s == NT:
+                for c in TURNED_LAST:
+                    scale(s - 1, c, nc.scalar)
             if s < NT:
+                scale(s - 1, 0, nc.scalar)
                 scale(s - 1, 1, nc.scalar, 0, 3)
                 mean(s)
                 scale(s - 1, 1, nc.scalar, 3)

@@ -37,7 +37,8 @@ def tile_multiheadattention_pb_kernel(tc, attn_out, residual, proj_w, proj_b, ln
     nc = tc.nc
     with ExitStack() as ctx:
         keep = ctx.enter_context(tc.tile_pool(name="keep", bufs=1))
-        x_pool = ctx.enter_context(tc.tile_pool(name="x_pool", bufs=NT // 2))
+        x_pool = ctx.enter_context(tc.tile_pool(name="x_pool", bufs=1))
+        x1_pool = ctx.enter_context(tc.tile_pool(name="x1_pool", bufs=NT - 2))
         w_pool = ctx.enter_context(tc.tile_pool(name="w_pool", bufs=NC))
         work = ctx.enter_context(tc.tile_pool(name="work", bufs=3))
         rb_pool = ctx.enter_context(tc.tile_pool(name="rb_pool", bufs=5))
@@ -71,6 +72,10 @@ def tile_multiheadattention_pb_kernel(tc, attn_out, residual, proj_w, proj_b, ln
                 in_=x_view[:, :, t0 : t0 + 2, :].rearrange("p h t j -> p h (t j)"),
             )
 
+        def load_x1(t):
+            x_raw[t] = x1_pool.tile([P, H, DV], BF16, name="x_one")
+            nc.sync.dma_start(out=x_raw[t][:], in_=x_view[:, :, t, :])
+
         def load_w(c):
             cols = slice(c * BANK, (c + 1) * BANK)
             w_raw[c] = w_pool.tile([P, H, BANK], BF16, name="w_chunk")
@@ -85,10 +90,13 @@ def tile_multiheadattention_pb_kernel(tc, attn_out, residual, proj_w, proj_b, ln
         load_w(2)
         load_w(3)
         load_r(0)
-        load_x(2)
+        load_x1(2)
+        load_x1(3)
         load_r(1)
-        load_x(4)
-        load_x(6)
+        load_x1(4)
+        load_x1(5)
+        load_x1(6)
+        load_x1(7)
         load_r(2)
         nc.sync.dma_start(out=shift_bc[:], in_=ln_b.partition_broadcast(P))
         for t in range(3, NT):
@@ -99,13 +107,13 @@ def tile_multiheadattention_pb_kernel(tc, attn_out, residual, proj_w, proj_b, ln
         eps = keep.tile([P, 1], F32)
         nc.vector.memset(eps[:], LN_EPS)
         warm = keep.tile([P, 1], F32)
-        nc.scalar.activation(out=warm[:], in_=eps[:], func=ACT.Sqrt)
+        nc.scalar.activation(out=warm[:], in_=eps[:], func=ACT.Abs_reciprocal_sqrt)
         ident_b = keep.tile([P, P], BF16)
         make_identity(nc, ident_b[:])
         ident_f = keep.tile([P, P], F32)
         make_identity(nc, ident_f[:])
 
-        x_words = keep.tile([P, NT, 2, P], F32)
+        x_words = keep.tile([P, 2, 2, P], F32)
         x_grouped = keep.tile([P, NT, P, H], BF16, align_bytes=64)
         x_codes = keep.tile([P, NT * P], U32, align_bytes=64)
         x_scales = keep.tile([P, NT * P], U8, align_bytes=64)
@@ -130,7 +138,11 @@ def tile_multiheadattention_pb_kernel(tc, attn_out, residual, proj_w, proj_b, ln
             xt = psum_c.tile([P, 2, 2, P], F32, name="xt", tag="c")
             for t in range(2):
                 for u in range(2):
-                    nc.tensor.transpose(xt[:, t, u, :], x_words[:, t0 + t, u, :], ident_f[:])
+                    if t0 == 0:
+                        words = x_words[:, t, u, :]
+                    else:
+                        words = x_raw[t0 + t][:].rearrange("p h j -> p (h j)").bitcast(F32)[:, u::2]
+                    nc.tensor.transpose(xt[:, t, u, :], words, ident_f[:])
             nc.scalar.copy(
                 out=x_grouped_pair(t0).bitcast(F32).rearrange("q (t p u) -> q t p u", t=2, u=2),
                 in_=xt[:].rearrange("q t u p -> q t p u"),
@@ -192,7 +204,6 @@ def tile_multiheadattention_pb_kernel(tc, attn_out, residual, proj_w, proj_b, ln
         z_of = {}
         neg_mean_of = {}
         sq_sum_of = {}
-        std_of = {}
         centred_of = {}
         turned_of = {}
         scaled_of = {}
@@ -214,7 +225,10 @@ def tile_multiheadattention_pb_kernel(tc, attn_out, residual, proj_w, proj_b, ln
         def multiply(i, c):
             toks = slice(i * P, (i + 1) * P)
             cols = slice(c * BANK, (c + 1) * BANK)
-            z_of[i, c] = psum_z.tile([P, BANK], F32, name="z", tag="z")
+            if (i, c) == (0, 3):
+                z_of[i, c] = psum_o.tile([P, BANK], F32, name="z_head", tag="o")
+            else:
+                z_of[i, c] = psum_z.tile([P, BANK], F32, name="z", tag="z")
             for again in range(REPEATS[min(i, 1)]):
                 nc.tensor.matmul_mx(
                     out=z_of[i, c][:],
@@ -227,7 +241,7 @@ def tile_multiheadattention_pb_kernel(tc, attn_out, residual, proj_w, proj_b, ln
                 )
 
         def add(i, c):
-            if c == 0:
+            if i not in y_of:
                 y_of[i] = pairs.tile([P, D], F32, name="y")
                 sums_of[i] = small.tile([P, NC], F32, name="sums")
             cols = slice(c * BANK, (c + 1) * BANK)
@@ -268,12 +282,10 @@ def tile_multiheadattention_pb_kernel(tc, attn_out, residual, proj_w, proj_b, ln
             sq_sum_of[i] = sq_sum
 
         def root(i):
-            std_of[i] = small.tile([P, 1], F32, name="std")
-            nc.scalar.activation(out=std_of[i][:], in_=sq_sum_of[i][:], func=ACT.Sqrt, bias=eps[:], scale=1.0 / D)
-
-        def invert(i):
             rstd_of[i] = small.tile([P, 1], F32, name="rstd")
-            nc.vector.reciprocal(out=rstd_of[i][:], in_=std_of[i][:])
+            nc.scalar.activation(
+                out=rstd_of[i][:], in_=sq_sum_of[i][:], func=ACT.Abs_reciprocal_sqrt, bias=eps[:], scale=1.0 / D
+            )
 
         def keep_clock(bank):
             nc.tensor.matmul(out=bank, lhsT=ident_f[:], rhs=ident_f[:], start=True, stop=True)
@@ -428,12 +440,11 @@ def tile_multiheadattention_pb_kernel(tc, attn_out, residual, proj_w, proj_b, ln
         w_quantise(1)
         multiply(0, 1)
         w_quantise(3)
-        for t in range(2, NT):
-            x_order(t, nc.scalar.copy)
         x_turn(2)
         x_turn(4)
         x_turn(6)
-        residual_and_bias(0, nc.vector)
+        residual_and_bias(0, nc.gpsimd, (3,))
+        residual_and_bias(0, nc.vector, (0, 2, 1))
         add(0, 0)
         multiply(0, 3)
         add(0, 2)
@@ -496,7 +507,6 @@ def tile_multiheadattention_pb_kernel(tc, attn_out, residual, proj_w, proj_b, ln
                 store(s - 2, 0, 2)
             if s < NT:
                 add(s, 3)
-                invert(s - 1)
                 turn_back(s - 1, 2)
             if s == NT:
                 for c in TURNED_LAST:
@@ -509,7 +519,6 @@ def tile_multiheadattention_pb_kernel(tc, attn_out, residual, proj_w, proj_b, ln
             if s + 1 < NT:
                 multiply(s + 1, 1)
                 multiply(s + 1, 2)
-        invert(NT - 1)
         for c in TURNED_LAST:
             turn_back(NT - 1, c)
         for c in range(len(TURNED_LAST), NC):

@@ -442,13 +442,13 @@ def tile_multiheadattention_pb_kernel(tc, attn_out, residual, proj_w, proj_b, ln
         w_quantise(3)
         x_turn(2)
         x_turn(4)
-        x_turn(6)
         residual_and_bias(0, nc.gpsimd, (3,))
         residual_and_bias(0, nc.vector, (0, 2, 1))
         add(0, 0)
         multiply(0, 3)
         add(0, 2)
         add(0, 1)
+        x_turn(6)
         add(0, 3)
         x_quantise(2)
         multiply(1, 0)
@@ -457,71 +457,93 @@ def tile_multiheadattention_pb_kernel(tc, attn_out, residual, proj_w, proj_b, ln
         residual_and_bias(1, nc.gpsimd, range(NC))
 
         mean(0)
-        for s in range(1, NT + 1):
+        for s in range(1, NT - 1):
             centre(s - 1)
-            if s + 1 < NT:
-                residual_and_bias(s + 1, nc.gpsimd)
-            if s < NT:
-                turn_half(s - 1, 2)
+            residual_and_bias(s + 1, nc.gpsimd)
+            turn_half(s - 1, 2)
             deviation(s - 1)
             if s == 1:
                 x_quantise(4)
             if s == 2:
                 x_quantise(6)
-            if s < NT:
-                add(s, 0)
+            add(s, 0)
             if s >= 2:
                 finish_direct(s - 2)
                 finish(s - 2, 2)
                 store(s - 2, 2, 4)
                 turn_back(s - 2, 0)
-                if s == NT:
-                    turn_half(NT - 1, 0)
                 turn_back(s - 2, 1)
-                if s == NT:
-                    for c in TURNED_LAST[1:]:
-                        turn_half(NT - 1, c)
-            if s < NT:
-                add(s, 1)
-                gain_direct(s - 1)
-                multiply(s, 3)
-            else:
-                scale_last(s - 1)
-            if s + 1 < NT:
-                multiply(s + 1, 0)
+            add(s, 1)
+            gain_direct(s - 1)
+            multiply(s, 3)
+            multiply(s + 1, 0)
             if s >= 2:
                 finish(s - 2, 0)
-            if s < NT:
-                add(s, 2)
-            if s < NT:
-                turn_half(s - 1, 0)
-            if s < NT:
-                scale(s - 1, 2, nc.scalar, 0, 2)
+            add(s, 2)
+            turn_half(s - 1, 0)
+            scale(s - 1, 2, nc.scalar, 0, 2)
             root(s - 1)
-            if s < NT:
-                scale(s - 1, 2, nc.scalar, 2)
-            if s < NT:
-                turn_half(s - 1, 1)
+            scale(s - 1, 2, nc.scalar, 2)
+            turn_half(s - 1, 1)
             if s >= 2:
                 finish(s - 2, 1)
                 store(s - 2, 0, 2)
-            if s < NT:
-                add(s, 3)
-                turn_back(s - 1, 2)
-            if s == NT:
-                for c in TURNED_LAST:
-                    scale(s - 1, c, nc.scalar)
-            if s < NT:
-                scale(s - 1, 0, nc.scalar)
-                scale(s - 1, 1, nc.scalar, 0, 3)
-                mean(s)
-                scale(s - 1, 1, nc.scalar, 3)
-            if s + 1 < NT:
-                multiply(s + 1, 1)
-                multiply(s + 1, 2)
-        for c in TURNED_LAST:
-            turn_back(NT - 1, c)
-        for c in range(len(TURNED_LAST), NC):
-            finish_last(NT - 1, c)
-        for c in TURNED_LAST:
-            finish(NT - 1, c)
+            add(s, 3)
+            turn_back(s - 1, 2)
+            scale(s - 1, 0, nc.scalar)
+            scale(s - 1, 1, nc.scalar, 0, 3)
+            mean(s)
+            scale(s - 1, 1, nc.scalar, 3)
+            multiply(s + 1, 1)
+            multiply(s + 1, 2)
+        k, m, z = NT - 3, NT - 2, NT - 1
+        finish_direct(k)
+        centre(m)
+        turn_half(m, 2)
+        deviation(m)
+        finish(k, 2)
+        add(z, 0)
+        store(k, 2, 4)
+        turn_back(k, 0)
+        turn_back(k, 1)
+        add(z, 1)
+        gain_direct(m)
+        multiply(z, 3)
+        turn_half(m, 0)
+        add(z, 2)
+        scale(m, 2, nc.scalar, 0, 2)
+        scale(m, 2, nc.scalar, 2)
+        finish(k, 0)
+        turn_half(m, 1)
+        finish(k, 1)
+        store(k, 0, 2)
+        add(z, 3)
+        turn_back(m, 2)
+        root(m)
+        scale(m, 0, nc.scalar)
+        scale(m, 1, nc.scalar, 3)
+        mean(z)
+        scale(m, 1, nc.scalar, 0, 3)
+        deviation(z)
+        finish_direct(m)
+        store(m, 3, 4)
+        finish(m, 2)
+        store(m, 2, 3)
+        turn_back(m, 0)
+        turn_half(z, 0)
+        turn_back(m, 1)
+        turn_half(z, 1)
+        scale_last(z)
+        finish(m, 0)
+        store(m, 0, 1)
+        root(z)
+        finish(m, 1)
+        store(m, 1, 2)
+        scale(z, 0, nc.scalar)
+        scale(z, 1, nc.scalar)
+        turn_back(z, 0)
+        turn_back(z, 1)
+        finish_last(z, 2)
+        finish_last(z, 3)
+        finish(z, 0)
+        finish(z, 1)

from contextlib import ExitStack

import concourse.mybir as mybir
from concourse.masks import make_identity

F32 = mybir.dt.float32
BF16 = mybir.dt.bfloat16
U32 = mybir.dt.uint32
U8 = mybir.dt.uint8
FP8X4 = mybir.dt.float8_e4m3fn_x4
ALU = mybir.AluOpType
ACT = mybir.ActivationFunctionType

P = 128
H = 4
DV = 128
LQ = 1024
D = 2048
NT = LQ // P
NF = D // P
BANK = 512
NC = D // BANK
F_PER_CHUNK = BANK // P
LN_EPS = 1e-5
CHUNK_ORDER = (2, 0, 1)
DIRECT = 3
HALF = 2
CENTRING = {2: ("product", "scalar"), 0: ("product", "transpose"), 1: ("transpose", "transpose")}
TURNED_LAST = (0, 1)
CENTRING_LAST = ("transpose", "transpose")
REPEATS = (1, 1)

FLOPS = 2 * LQ * H * DV * D


def tile_multiheadattention_pb_kernel(tc, attn_out, residual, proj_w, proj_b, ln_g, ln_b, out):
    nc = tc.nc
    with ExitStack() as ctx:
        keep = ctx.enter_context(tc.tile_pool(name="keep", bufs=1))
        x_pool = ctx.enter_context(tc.tile_pool(name="x_pool", bufs=1))
        x1_pool = ctx.enter_context(tc.tile_pool(name="x1_pool", bufs=NT - 2))
        w_pool = ctx.enter_context(tc.tile_pool(name="w_pool", bufs=NC))
        work = ctx.enter_context(tc.tile_pool(name="work", bufs=3))
        rb_pool = ctx.enter_context(tc.tile_pool(name="rb_pool", bufs=5))
        cols_pool = ctx.enter_context(tc.tile_pool(name="cols_pool", bufs=8))
        pairs = ctx.enter_context(tc.tile_pool(name="pairs", bufs=2))
        small = ctx.enter_context(tc.tile_pool(name="small", bufs=4))
        psum_k = ctx.enter_context(tc.psum_pool(name="psum_k", bufs=1))
        psum_z = ctx.enter_context(tc.psum_pool(name="psum_z", bufs=3))
        psum_c = ctx.enter_context(tc.psum_pool(name="psum_c", bufs=2))
        psum_o = ctx.enter_context(tc.psum_pool(name="psum_o", bufs=2))

        vec_rows = keep.tile([P, P], BF16)
        nc.vector.memset(vec_rows[:], 0.0)
        nc.sync.dma_start(out=vec_rows[0:NF, :], in_=proj_b.rearrange("(j q) -> j q", q=P))
        nc.sync.dma_start(out=vec_rows[NF : 2 * NF, :], in_=ln_g.rearrange("(j q) -> j q", q=P))
        nc.sync.dma_start(out=vec_rows[2 * NF : 3 * NF, :], in_=ln_b.rearrange("(j q) -> j q", q=P))
        bias_bc = keep.tile([P, D], BF16)
        x_raw = {}
        x_view = attn_out.rearrange("h (p t) j -> p h t j", t=NT)
        w_raw = {}
        w_view = proj_w.rearrange("(q i) n -> q i n", i=H)
        r_sb = keep.tile([P, NT, D], BF16)
        r_view = residual.rearrange("(p t) n -> p t n", t=NT)
        shift_bc = keep.tile([P, D], BF16)
        gain_bc = keep.tile([P, D], BF16)

        def load_x(t0):
            x_raw[t0] = x_pool.tile([P, H, 2, DV], BF16, name="x_pair")
            nc.sync.dma_start(
                out=x_raw[t0][:].rearrange("p h t j -> p h (t j)"),
                in_=x_view[:, :, t0 : t0 + 2, :].rearrange("p h t j -> p h (t j)"),
            )

        def load_x1(t):
            x_raw[t] = x1_pool.tile([P, H, DV], BF16, name="x_one")
            nc.sync.dma_start(out=x_raw[t][:], in_=x_view[:, :, t, :])

        def load_w(c):
            cols = slice(c * BANK, (c + 1) * BANK)
            w_raw[c] = w_pool.tile([P, H, BANK], BF16, name="w_chunk")
            nc.sync.dma_start(out=w_raw[c][:], in_=w_view[:, :, cols])

        def load_r(t):
            nc.sync.dma_start(out=r_sb[:, t, :], in_=r_view[:, t, :])

        load_x(0)
        load_w(0)
        load_w(1)
        load_w(2)
        load_w(3)
        load_r(0)
        load_x1(2)
        load_x1(3)
        load_r(1)
        load_x1(4)
        load_x1(5)
        load_x1(6)
        load_x1(7)
        load_r(2)
        nc.sync.dma_start(out=shift_bc[:], in_=ln_b.partition_broadcast(P))
        for t in range(3, NT):
            load_r(t)

        nc.sync.dma_start(out=gain_bc[:], in_=ln_g.partition_broadcast(P))

        eps = keep.tile([P, 1], F32)
        nc.vector.memset(eps[:], LN_EPS)
        warm = keep.tile([P, 1], F32)
        nc.scalar.activation(out=warm[:], in_=eps[:], func=ACT.Abs_reciprocal_sqrt)
        ident_b = keep.tile([P, P], BF16)
        make_identity(nc, ident_b[:])
        ident_f = keep.tile([P, P], F32)
        make_identity(nc, ident_f[:])

        x_words = keep.tile([P, 2, 2, P], F32)
        x_grouped = keep.tile([P, NT, P, H], BF16, align_bytes=64)
        x_codes = keep.tile([P, NT * P], U32, align_bytes=64)
        x_scales = keep.tile([P, NT * P], U8, align_bytes=64)
        w_grouped = {}
        w_codes = keep.tile([P, D], U32, align_bytes=64)
        w_scales = keep.tile([P, D], U8, align_bytes=64)
        bias_col = keep.tile([P, NF], BF16)
        vec_col = keep.tile([P, 2 * NF], BF16)
        gain_col = keep.tile([P, NF], F32)
        out_view = out.rearrange("(p t) n -> p t n", t=NT)

        def x_order(t, copy):
            copy(
                out=x_words[:, t, :, :].rearrange("p u (h a) -> p u h a", h=H),
                in_=x_raw[t - t % 2][:, :, t % 2, :].bitcast(F32).rearrange("p h (a u) -> p u h a", u=2),
            )

        def x_grouped_pair(t0):
            return x_grouped[:, t0 : t0 + 2, :, :].rearrange("q t p i -> q (t p i)")

        def x_turn(t0):
            xt = psum_c.tile([P, 2, 2, P], F32, name="xt", tag="c")
            for t in range(2):
                for u in range(2):
                    if t0 == 0:
                        words = x_words[:, t, u, :]
                    else:
                        words = x_raw[t0 + t][:].rearrange("p h j -> p (h j)").bitcast(F32)[:, u::2]
                    nc.tensor.transpose(xt[:, t, u, :], words, ident_f[:])
            nc.scalar.copy(
                out=x_grouped_pair(t0).bitcast(F32).rearrange("q (t p u) -> q t p u", t=2, u=2),
                in_=xt[:].rearrange("q t u p -> q t p u"),
            )

        def x_quantise(t0):
            toks = slice(t0 * P, (t0 + 2) * P)
            nc.vector.quantize_mx(out=x_codes[:, toks].bitcast(FP8X4), scales=x_scales[:, toks], in_=x_grouped_pair(t0))

        def w_group(c, copy, first=0, last=BANK):
            if c not in w_grouped:
                w_grouped[c] = w_pool.tile([P, BANK, H], BF16, name="w_words", align_bytes=64)
            copy(
                out=w_grouped[c][:, first:last, :].rearrange("q (m n) i -> q m i n", n=4),
                in_=w_raw[c][:, :, first:last].rearrange("q i (m n) -> q m i n", n=4),
            )

        def w_quantise(c):
            cols = slice(c * BANK, (c + 1) * BANK)
            nc.vector.quantize_mx(
                out=w_codes[:, cols].bitcast(FP8X4),
                scales=w_scales[:, cols],
                in_=w_grouped[c][:].rearrange("q n i -> q (n i)"),
            )

        def turn_vectors():
            rows_ps = psum_o.tile([P, P], BF16, name="rows_ps", tag="o")
            nc.tensor.transpose(rows_ps[:], vec_rows[:], ident_b[:])
            nc.vector.tensor_copy(out=bias_col[:], in_=rows_ps[:, 0:NF])
            nc.vector.tensor_copy(out=gain_col[:], in_=rows_ps[:, NF : 2 * NF])
            nc.vector.tensor_copy(out=vec_col[:], in_=rows_ps[:, NF : 3 * NF])

        spread_of = {}

        def spread_bias(half):
            spread_of[half] = psum_o.tile([P, D // 2], BF16, name="spread", tag="o")
            for k in range(NF // 2):
                j = half * (NF // 2) + k
                nc.tensor.transpose(
                    spread_of[half][:, k * P : (k + 1) * P], bias_col[:, j : j + 1].to_broadcast([P, P]), ident_b[:]
                )

        direct = psum_k.tile([P, 2, BANK], BF16, name="direct")

        def spread_direct():
            for v in range(2):
                for jj in range(F_PER_CHUNK):
                    j = v * NF + DIRECT * F_PER_CHUNK + jj
                    nc.tensor.transpose(
                        direct[:, v, jj * P : (jj + 1) * P], vec_col[:, j : j + 1].to_broadcast([P, P]), ident_b[:]
                    )

        def keep_bias(half):
            nc.scalar.copy(out=bias_bc[:, half * (D // 2) : (half + 1) * (D // 2)], in_=spread_of[half][:])

        rb_of = {}
        y_of = {}
        sums_of = {}
        z_of = {}
        neg_mean_of = {}
        sq_sum_of = {}
        centred_of = {}
        turned_of = {}
        scaled_of = {}
        rstd_of = {}
        back_of = {}
        o_of = {}

        def residual_and_bias(i, engine, chunks=range(NC)):
            if i not in rb_of:
                rb_of[i] = rb_pool.tile([P, D], F32, name="rb")
            for c in chunks:
                cols = slice(c * BANK, (c + 1) * BANK)
                if engine is nc.vector:
                    bias = spread_of[c // 2][:, c % 2 * BANK : (c % 2 + 1) * BANK]
                else:
                    bias = bias_bc[:, cols]
                engine.tensor_tensor(out=rb_of[i][:, cols], in0=r_sb[:, i, cols], in1=bias, op=ALU.add)

        def multiply(i, c):
            toks = slice(i * P, (i + 1) * P)
            cols = slice(c * BANK, (c + 1) * BANK)
            if (i, c) == (0, 3):
                z_of[i, c] = psum_o.tile([P, BANK], F32, name="z_head", tag="o")
            else:
                z_of[i, c] = psum_z.tile([P, BANK], F32, name="z", tag="z")
            for again in range(REPEATS[min(i, 1)]):
                nc.tensor.matmul_mx(
                    out=z_of[i, c][:],
                    lhsT=x_codes[:, toks].bitcast(FP8X4),
                    lhsT_scale=x_scales[:, toks],
                    rhs=w_codes[:, cols].bitcast(FP8X4),
                    rhs_scale=w_scales[:, cols],
                    start=True,
                    stop=True,
                )

        def add(i, c):
            if i not in y_of:
                y_of[i] = pairs.tile([P, D], F32, name="y")
                sums_of[i] = small.tile([P, NC], F32, name="sums")
            cols = slice(c * BANK, (c + 1) * BANK)
            nc.vector.scalar_tensor_tensor(
                out=y_of[i][:, cols],
                in0=z_of[i, c][:],
                scalar=0.0,
                in1=rb_of[i][:, cols],
                op0=ALU.add,
                op1=ALU.add,
                accum_out=sums_of[i][:, c : c + 1],
            )

        def mean(i):
            neg_mean = neg_mean_of[i] = small.tile([P, 1], F32, name="neg_mean")
            parts = small.tile([P, NC], F32, name="parts")
            nc.scalar.activation(
                out=parts[:], in_=sums_of[i][:], func=ACT.Copy, scale=-1.0 / D, accum_out=neg_mean[:]
            )

        def centre(i):
            neg_mean = neg_mean_of[i]
            centred_of[i] = pairs.tile([P, D], F32, name="centred")
            for c in CHUNK_ORDER:
                for h in range(2):
                    if i < NT - 1 and CENTRING[c][h] == "scalar":
                        cols = slice(c * BANK + h * HALF * P, c * BANK + (h + 1) * HALF * P)
                        nc.scalar.activation(
                            out=centred_of[i][:, cols], in_=y_of[i][:, cols], func=ACT.Identity, bias=neg_mean[:], scale=1.0
                        )

        def deviation(i):
            squares = pairs.tile([P, D], BF16, name="squares")
            sq_sum = small.tile([P, 1], F32, name="sq_sum")
            nc.scalar.activation(
                out=squares[:], in_=y_of[i][:], func=ACT.Square, bias=neg_mean_of[i][:], scale=1.0, accum_out=sq_sum[:]
            )
            sq_sum_of[i] = sq_sum

        def root(i):
            rstd_of[i] = small.tile([P, 1], F32, name="rstd")
            nc.scalar.activation(
                out=rstd_of[i][:], in_=sq_sum_of[i][:], func=ACT.Abs_reciprocal_sqrt, bias=eps[:], scale=1.0 / D
            )

        def keep_clock(bank):
            nc.tensor.matmul(out=bank, lhsT=ident_f[:], rhs=ident_f[:], start=True, stop=True)

        def turn_half(i, c):
            turned_of[i, c] = psum_c.tile([P, F_PER_CHUNK, P], F32, name="turned", tag="c")
            for h in range(2):
                way = CENTRING[c][h] if i < NT - 1 else CENTRING_LAST[h]
                tiles = range(h * HALF, (h + 1) * HALF)
                source = centred_of[i] if way == "scalar" else y_of[i]
                for jj in tiles:
                    j = c * F_PER_CHUNK + jj
                    nc.tensor.matmul(
                        out=turned_of[i, c][:, jj, :],
                        lhsT=source[:, j * P : (j + 1) * P],
                        rhs=ident_f[:],
                        start=(jj == tiles[0]),
                        stop=(way == "scalar" and jj == tiles[-1]),
                        is_transpose=True,
                    )
                spread_mean = neg_mean_of[i][:].to_broadcast([P, P])
                if way == "product":
                    nc.tensor.matmul(
                        out=turned_of[i, c][:, h * HALF : (h + 1) * HALF, :],
                        lhsT=spread_mean,
                        rhs=ident_f[:].unsqueeze(1).to_broadcast([P, HALF, P]),
                        start=False,
                        stop=True,
                    )
                if way == "transpose":
                    for jj in tiles:
                        nc.tensor.matmul(
                            out=turned_of[i, c][:, jj, :],
                            lhsT=spread_mean,
                            rhs=ident_f[:],
                            start=False,
                            stop=(jj == tiles[-1]),
                            is_transpose=True,
                        )

        def scale(i, c, engine, first=0, last=F_PER_CHUNK):
            if (i, c) not in scaled_of:
                scaled_of[i, c] = cols_pool.tile([P, F_PER_CHUNK, P], F32, name="scaled")
            if engine is nc.vector:
                gains = gain_col[:, c * F_PER_CHUNK + first : c * F_PER_CHUNK + last]
                nc.vector.tensor_tensor(
                    out=scaled_of[i, c][:, first:last, :],
                    in0=turned_of[i, c][:, first:last, :],
                    in1=gains.unsqueeze(2).to_broadcast([P, last - first, P]),
                    op=ALU.mult,
                )
                return
            for jj in range(first, last):
                j = c * F_PER_CHUNK + jj
                nc.scalar.activation(
                    out=scaled_of[i, c][:, jj, :], in_=turned_of[i, c][:, jj, :], func=ACT.Copy, scale=gain_col[:, j : j + 1]
                )

        def turn_back(i, c, warm=False):
            back_of[i, c] = psum_o.tile([P, BANK], F32, name="back", tag="o")
            if warm:
                keep_clock(back_of[i, c][:, 0:P])
            for jj in range(F_PER_CHUNK):
                nc.tensor.transpose(back_of[i, c][:, jj * P : (jj + 1) * P], scaled_of[i, c][:, jj, :], ident_f[:])

        def scale_last(i):
            o_of[i] = work.tile([P, D], F32, name="o")
            cols = slice(len(TURNED_LAST) * BANK, D)
            nc.vector.scalar_tensor_tensor(
                out=o_of[i][:, cols],
                in0=y_of[i][:, cols],
                scalar=neg_mean_of[i][:],
                in1=gain_bc[:, cols],
                op0=ALU.add,
                op1=ALU.mult,
            )

        def gain_direct(i):
            o_of[i] = work.tile([P, D], F32, name="o")
            cols = slice(DIRECT * BANK, (DIRECT + 1) * BANK)
            nc.vector.scalar_tensor_tensor(
                out=o_of[i][:, cols],
                in0=y_of[i][:, cols],
                scalar=neg_mean_of[i][:],
                in1=direct[:, 0, :],
                op0=ALU.add,
                op1=ALU.mult,
            )

        def finish_direct(i):
            cols = slice(DIRECT * BANK, (DIRECT + 1) * BANK)
            nc.vector.scalar_tensor_tensor(
                out=o_of[i][:, cols],
                in0=o_of[i][:, cols],
                scalar=rstd_of[i][:],
                in1=direct[:, 1, :],
                op0=ALU.mult,
                op1=ALU.add,
            )

        def store(i, first, last):
            cols = slice(first * BANK, last * BANK)
            nc.sync.dma_start(out=out_view[:, i, cols], in_=o_of[i][:, cols])

        def finish_last(i, c):
            cols = slice(c * BANK, (c + 1) * BANK)
            nc.vector.scalar_tensor_tensor(
                out=o_of[i][:, cols],
                in0=o_of[i][:, cols],
                scalar=rstd_of[i][:],
                in1=shift_bc[:, cols],
                op0=ALU.mult,
                op1=ALU.add,
            )
            nc.sync.dma_start(out=out_view[:, i, cols], in_=o_of[i][:, cols])

        def finish(i, c):
            if i not in o_of:
                o_of[i] = work.tile([P, D], F32, name="o")
            cols = slice(c * BANK, (c + 1) * BANK)
            nc.vector.scalar_tensor_tensor(
                out=o_of[i][:, cols],
                in0=back_of[i, c][:],
                scalar=rstd_of[i][:],
                in1=shift_bc[:, cols],
                op0=ALU.mult,
                op1=ALU.add,
            )
            if i == NT - 1:
                store(i, c, c + 1)

        ctx.enter_context(tc.manual_schedule())
        x_order(0, nc.vector.tensor_copy)
        x_order(1, nc.vector.tensor_copy)
        turn_vectors()
        x_turn(0)
        spread_bias(0)
        spread_bias(1)
        spread_direct()
        w_group(0, nc.vector.tensor_copy)
        w_quantise(0)
        w_group(1, nc.scalar.copy)
        x_quantise(0)
        multiply(0, 0)
        w_group(2, nc.vector.tensor_copy)
        w_quantise(2)
        multiply(0, 2)
        w_group(3, nc.vector.tensor_copy, 0, 256)
        w_group(3, nc.scalar.copy, 256, BANK)
        keep_bias(0)
        keep_bias(1)
        w_quantise(1)
        multiply(0, 1)
        w_quantise(3)
        x_turn(2)
        x_turn(4)
        residual_and_bias(0, nc.gpsimd, (3,))
        residual_and_bias(0, nc.vector, (0, 2, 1))
        add(0, 0)
        multiply(0, 3)
        add(0, 2)
        add(0, 1)
        x_turn(6)
        add(0, 3)
        x_quantise(2)
        multiply(1, 0)
        multiply(1, 1)
        multiply(1, 2)
        residual_and_bias(1, nc.gpsimd, range(NC))

        mean(0)
        for s in range(1, NT - 1):
            centre(s - 1)
            residual_and_bias(s + 1, nc.gpsimd)
            turn_half(s - 1, 2)
            deviation(s - 1)
            if s == 1:
                x_quantise(4)
            if s == 2:
                x_quantise(6)
            add(s, 0)
            if s >= 2:
                finish_direct(s - 2)
                finish(s - 2, 2)
                store(s - 2, 2, 4)
                turn_back(s - 2, 0)
                turn_back(s - 2, 1)
            add(s, 1)
            gain_direct(s - 1)
            multiply(s, 3)
            multiply(s + 1, 0)
            if s >= 2:
                finish(s - 2, 0)
            add(s, 2)
            turn_half(s - 1, 0)
            scale(s - 1, 2, nc.scalar, 0, 2)
            root(s - 1)
            scale(s - 1, 2, nc.scalar, 2)
            turn_half(s - 1, 1)
            if s >= 2:
                finish(s - 2, 1)
                store(s - 2, 0, 2)
            add(s, 3)
            turn_back(s - 1, 2)
            scale(s - 1, 0, nc.scalar)
            scale(s - 1, 1, nc.scalar, 0, 3)
            mean(s)
            scale(s - 1, 1, nc.scalar, 3)
            multiply(s + 1, 1)
            multiply(s + 1, 2)
        k, m, z = NT - 3, NT - 2, NT - 1
        finish_direct(k)
        centre(m)
        turn_half(m, 2)
        deviation(m)
        finish(k, 2)
        add(z, 0)
        store(k, 2, 4)
        turn_back(k, 0)
        turn_back(k, 1)
        add(z, 1)
        gain_direct(m)
        multiply(z, 3)
        turn_half(m, 0)
        add(z, 2)
        scale(m, 2, nc.scalar, 0, 2)
        scale(m, 2, nc.scalar, 2)
        finish(k, 0)
        turn_half(m, 1)
        finish(k, 1)
        store(k, 0, 2)
        add(z, 3)
        turn_back(m, 2)
        root(m)
        scale(m, 0, nc.scalar)
        scale(m, 1, nc.scalar, 3)
        mean(z)
        scale(m, 1, nc.scalar, 0, 3)
        deviation(z)
        finish_direct(m)
        store(m, 3, 4)
        finish(m, 2)
        store(m, 2, 3)
        turn_back(m, 0)
        turn_half(z, 0)
        turn_back(m, 1)
        turn_half(z, 1)
        scale_last(z)
        finish(m, 0)
        store(m, 0, 1)
        root(z)
        finish(m, 1)
        store(m, 1, 2)
        scale(z, 0, nc.scalar)
        scale(z, 1, nc.scalar)
        turn_back(z, 0)
        turn_back(z, 1)
        finish_last(z, 2)
        finish_last(z, 3)
        finish(z, 0)
        finish(z, 1)
